import numpy as np
import ml_dtypes


def mxq(x, axis, fmt="e4m3"):
    dtype, down = {"e4m3": (ml_dtypes.float8_e4m3fn, 7), "e5m2": (ml_dtypes.float8_e5m2, 14)}[fmt]
    v = np.moveaxis(np.asarray(x, np.float32).astype(ml_dtypes.bfloat16).astype(np.float64), axis, -1)
    blocks = v.reshape(v.shape[:-1] + (-1, 32))
    amax = np.abs(blocks).max(-1, keepdims=True)
    byte = np.maximum(np.where(amax > 0, np.frexp(amax)[1] - 1 + 127, 0) - down, 1)
    scale = np.exp2(byte - 127.0)
    codes = (blocks / scale).astype(np.float32).astype(dtype).astype(np.float64)
    return np.moveaxis((codes * scale).reshape(v.shape), -1, axis)


WIDE = False


def mx_kscale(k):
    if not WIDE:
        return np.ones(k)
    levels = np.array([30, -30])
    if k % 512:
        return np.exp2(np.random.permutation(np.resize(levels, k // 32))).repeat(32)
    a = np.empty((k // 512, 16))
    for p in range(k // 512):
        a[p, :8] = np.random.permutation(np.resize(levels, 8))
        for g in range(8):
            far = levels[np.abs(levels - a[p, g]) >= 10]
            a[p, g + 8] = far[np.random.randint(len(far))]
    return np.exp2(a.ravel()).repeat(32)


BF16 = ml_dtypes.bfloat16


def bf(x):
    return np.asarray(x, np.float32).astype(BF16)


def f64(x):
    return np.asarray(x).astype(np.float64)


B, T, D, H, DH = 2, 256, 2048, 16, 128
E = H * DH
EPS = 1e-6
ROPE_BASE = 10000.0


def rms_norm(t):
    return t / np.sqrt(np.mean(t * t, axis=-1, keepdims=True) + EPS)


def rope(t):
    inv_freq = 1.0 / ROPE_BASE ** (np.arange(0, DH, 2) / DH)
    ang = np.arange(T)[:, None] * inv_freq[None, :]
    cos, sin = np.cos(ang), np.sin(ang)
    t1, t2 = t[..., :DH // 2], t[..., DH // 2:]
    return np.concatenate([t1 * cos - t2 * sin, t1 * sin + t2 * cos], axis=-1)


def setup_inputs():
    s = mx_kscale(D)
    return {"x": bf(np.random.standard_normal((B, T, D)) * s),
            "W_qk": bf(np.random.standard_normal((D, 2 * E)) / np.sqrt(D) / s[:, None])}


def reference(x, W_qk):
    qk = mxq(f64(x), 2, "e5m2") @ mxq(f64(W_qk), 0, "e5m2")
    qk = qk.reshape(B, T, 2, H, DH).transpose(2, 0, 3, 1, 4)
    q, k = rms_norm(qk[0]), rms_norm(qk[1])
    return rope(q), rope(k)

@@ -1,0 +1,322 @@
+from contextlib import ExitStack
+import math
+
+import concourse.mybir as mybir
+from concourse.masks import make_identity
+
+FLOPS = 2 * 512 * 2048 * 4096
+
+F32 = mybir.dt.float32
+BF16 = mybir.dt.bfloat16
+U32 = mybir.dt.uint32
+U8 = mybir.dt.uint8
+I32 = mybir.dt.int32
+FP8X4 = mybir.dt.float8_e5m2_x4
+ALU = mybir.AluOpType
+ACT = mybir.ActivationFunctionType
+
+P = 128
+EPS = 1e-6
+N_TILES = 32
+V_HEAD = 256
+V_STEADY = 80
+V_LAST = 80
+ADD_ON_GPSIMD = True
+PT_COLS = 192
+PT_FIRST = 5
+PT_ON_VECTOR = False
+RSQRT_ON_SCALAR = True
+
+
+def tile_attn_pa_kernel(tc, x, W_qk, out_0, out_1):
+    nc = tc.nc
+    xf = x.flatten_outer_dims()
+    outs = (out_0, out_1)
+
+    with ExitStack() as ctx:
+        const = ctx.enter_context(tc.tile_pool(name="const", bufs=1))
+        xpool = ctx.enter_context(tc.tile_pool(name="xpool", bufs=1))
+        rawp = ctx.enter_context(tc.tile_pool(name="rawp", bufs=8))
+        grp = ctx.enter_context(tc.tile_pool(name="grp", bufs=3))
+        wqp = ctx.enter_context(tc.tile_pool(name="wqp", bufs=5))
+        small = ctx.enter_context(tc.tile_pool(name="small", bufs=4))
+        epi = ctx.enter_context(tc.tile_pool(name="epi", bufs=3))
+        psum = ctx.enter_context(tc.psum_pool(name="psum", bufs=6))
+        ctx.enter_context(tc.manual_schedule())
+
+        xraw = []
+        raw = {}
+
+        def load_x(m):
+            t = xpool.tile([P, 2048], BF16, name="xraw%d" % m)
+            nc.sync.dma_start(out=t[:], in_=xf[P * m : P * (m + 1), :])
+            xraw.append(t)
+
+        def load_w(key, c, col0, width):
+            t = rawp.tile([P, 4, width], BF16, name="raw", tag="raw")
+            nc.sync.dma_start(
+                out=t[:],
+                in_=W_qk[512 * c : 512 * (c + 1), col0 : col0 + width].rearrange("(p j) w -> p j w", j=4),
+            )
+            raw[key] = t
+
+        for c in range(4):
+            load_w((0, c), c, 0, 512)
+            load_x(c)
+        for c in range(4):
+            load_w((1, c), c, 512, 512)
+
+        def raw_of(k):
+            n, c = divmod(k, 4)
+            if n < 2:
+                return raw[(n, c)], 0
+            return raw[("pair", n // 2, c)], 512 * (n % 2)
+
+        ident = const.tile([P, P], F32, name="ident")
+        make_identity(nc, ident[:])
+        identb = const.tile([P, P], BF16, name="identb")
+        if PT_COLS:
+            nc.vector.tensor_copy(out=identb[:], in_=ident[:])
+        pcol = const.tile([P, 2], F32, name="pcol")
+        nc.gpsimd.iota(pcol[:], pattern=[[P, 2]], base=0, channel_multiplier=1, allow_small_or_imprecise_dtypes=True)
+        one = const.tile([P, 1], F32, name="one")
+        nc.vector.memset(one[:], 1.0)
+        warm = const.tile([P, 1], F32, name="warm")
+        nc.scalar.activation(out=warm[:], in_=one[:], func=ACT.Sin)
+        phi = const.tile([P, 64], F32, name="phi")
+        nc.vector.tensor_scalar(out=phi[:, 0:1], in0=one[:], scalar1=1.0 / (2.0 * math.pi), scalar2=None, op0=ALU.mult)
+        ratio = 10000.0 ** (-2.0 / 128.0)
+        for s in range(6):
+            w = 2 ** s
+            nc.vector.tensor_scalar(out=phi[:, w : 2 * w], in0=phi[:, 0:w], scalar1=ratio ** w, scalar2=None, op0=ALU.mult)
+        turns = const.tile([P, 2, 64], F32, name="turns")
+        for tt in range(2):
+            nc.vector.tensor_scalar(out=turns[:, tt, :], in0=phi[:], scalar1=pcol[:, tt : tt + 1], scalar2=None, op0=ALU.mult)
+        tf = turns[:].rearrange("p a c -> p (a c)")
+        ki = const.tile([P, 128], I32, name="ki")
+        nc.vector.tensor_copy(out=ki[:], in_=tf)
+        kf = const.tile([P, 128], F32, name="kf")
+        nc.vector.tensor_copy(out=kf[:], in_=ki[:])
+        fr = const.tile([P, 2, 64], F32, name="fr")
+        nc.vector.tensor_tensor(out=fr[:].rearrange("p a c -> p (a c)"), in0=tf, in1=kf[:], op=ALU.subtract)
+        ph = const.tile([P, 2, 4, 64], F32, name="ph")
+        for blk, off in enumerate((0.25, 0.25, 0.0, 0.5)):
+            nc.vector.tensor_scalar(out=ph[:, :, blk, :], in0=fr[:], scalar1=off, scalar2=None, op0=ALU.add)
+        phf = ph[:].rearrange("p a b c -> p (a b c)")
+        gm = const.tile([P, 512], F32, name="gm")
+        nc.vector.scalar_tensor_tensor(out=gm[:], in0=phf, scalar=0.5, in1=phf, op0=ALU.is_gt, op1=ALU.subtract)
+        cs = const.tile([P, 2, 2, P], F32, name="cs")
+
+        def tables_on_scalar():
+            nc.scalar.activation(out=cs[:].rearrange("p a b c -> p (a b c)"), in_=gm[:], func=ACT.Sin, scale=-2.0 * math.pi)
+            nc.scalar.activation(out=warm[:], in_=one[:], func=(ACT.Abs_reciprocal_sqrt if RSQRT_ON_SCALAR else ACT.Sqrt))
+
+        xq, xs, gxs = [], [], {}
+
+        def x_transpose(m):
+            words = xraw[m][:].bitcast(F32)
+            banks = []
+            for cp in range(2):
+                xt = psum.tile([P, 2, 2, P], F32, name="xt", tag="aux", bufs=2)
+                for cc in range(2):
+                    c = 2 * cp + cc
+                    for u in range(2):
+                        nc.tensor.transpose(out=xt[:, cc, u, :], in_=words[:, 256 * c + u : 256 * (c + 1) : 2], identity=ident[:])
+                banks.append(xt)
+            gx = xpool.tile([P, 4, P, 4], BF16, name="gx", tag="gx", bufs=2, align_bytes=64)
+            gxs[m] = (gx, banks)
+
+        def x_copy(m, cp, eng_copy):
+            gx, banks = gxs[m]
+            gw = gx[:].rearrange("p c r t -> p (c r t)").bitcast(F32).rearrange("p (c r u) -> p c r u", c=4, u=2)
+            eng_copy(out=gw[:, 2 * cp : 2 * cp + 2, :, :], in_=banks[cp][:].rearrange("p c u r -> p c r u"))
+
+        def x_quant(m):
+            gx, banks = gxs[m]
+            q = xpool.tile([P, 512], U32, name="xq%d" % m, align_bytes=64)
+            s = xpool.tile([P, 512], U8, name="xs%d" % m, align_bytes=64)
+            nc.vector.quantize_mx(out=q[:].bitcast(FP8X4), scales=s[:], in_=gx[:].rearrange("p c r t -> p (c r t)"))
+            xq.append(q)
+            xs.append(s)
+
+        grouped, wq, ws, acc = {}, {}, {}, {}
+
+        def v_cols(k):
+            return V_HEAD if k < 5 else (V_LAST if k >= 28 else V_STEADY)
+
+        def pt_cols(k):
+            return PT_COLS if PT_FIRST <= k < N_TILES else 0
+
+        pts = {}
+
+        def pass_through(k):
+            w = pt_cols(k)
+            if w == 0:
+                return
+            t, off = raw_of(k)
+            pt = psum.tile([P, 256, 4], BF16, name="pt", tag="aux", bufs=2)
+            for w0 in range(0, w, 128):
+                w1 = min(w, w0 + 128)
+                nc.tensor.matmul(
+                    out=pt[:, w0:w1, :],
+                    lhsT=identb[:],
+                    rhs=t[:, :, off + 512 - w + w0 : off + 512 - w + w1].rearrange("p j w -> p w j"),
+                    start=True,
+                    stop=True,
+                )
+            pts[k] = pt
+
+        def pt_evacuate(k):
+            w = pt_cols(k)
+            if w == 0:
+                return
+            if k not in grouped:
+                grouped[k] = grp.tile([P, 512, 4], BF16, name="grouped", tag="grouped", align_bytes=64)
+            if PT_ON_VECTOR:
+                nc.vector.tensor_copy(out=grouped[k][:, 512 - w : 512, :], in_=pts[k][:, 0:w, :])
+            else:
+                nc.scalar.copy(out=grouped[k][:, 512 - w : 512, :], in_=pts[k][:, 0:w, :])
+
+        def interleave(k, on_vector):
+            if k not in grouped:
+                grouped[k] = grp.tile([P, 512, 4], BF16, name="grouped", tag="grouped", align_bytes=64)
+            t, off = raw_of(k)
+            v = v_cols(k)
+            lo, hi = (0, v) if on_vector else (v, 512 - pt_cols(k))
+            if hi <= lo:
+                return
+            src = t[:, :, off + lo : off + hi].rearrange("p j w -> p w j")
+            if on_vector:
+                nc.vector.tensor_copy(out=grouped[k][:, lo:hi, :], in_=src)
+            else:
+                nc.scalar.copy(out=grouped[k][:, lo:hi, :], in_=src)
+
+        def quantize(k):
+            wq[k] = wqp.tile([P, 512], U32, name="wq", tag="wq", align_bytes=64)
+            ws[k] = wqp.tile([P, 512], U8, name="ws", tag="ws", align_bytes=64)
+            nc.vector.quantize_mx(out=wq[k][:].bitcast(FP8X4), scales=ws[k][:], in_=grouped[k][:].rearrange("p w j -> p (w j)"))
+
+        def one_pass(k, m):
+            n, c = divmod(k, 4)
+            e = 4 * n + m
+            if c == 0:
+                acc[e] = psum.tile([P, 512], F32, name="acc", tag="acc")
+            nc.tensor.matmul_mx(
+                out=acc[e][:],
+                lhsT=xq[m][:, P * c : P * (c + 1)].bitcast(FP8X4),
+                lhsT_scale=xs[m][:, P * c : P * (c + 1)],
+                rhs=wq[k][:].bitcast(FP8X4),
+                rhs_scale=ws[k][:],
+                start=(c == 0),
+                stop=(c == 3),
+            )
+
+        def passes(j):
+            c = j % 4
+            for m in range(c):
+                one_pass(j, m)
+            for cc in range(c + 1):
+                one_pass(j - c + cc, c)
+
+        rts, rs, abs_ = {}, {}, {}
+
+        def stats(e):
+            ss = small.tile([P, 4], F32, name="ss", tag="ss")
+            for h in range(4):
+                junk = small.tile([P, P], BF16, name="junk", tag="junk", bufs=2)
+                nc.scalar.activation(out=junk[:], in_=acc[e][:, P * h : P * (h + 1)], func=ACT.Square, accum_out=ss[:, h : h + 1])
+            rts[e] = small.tile([P, 4], F32, name="rt", tag="rt")
+            nc.scalar.activation(
+                out=rts[e][:], in_=ss[:], func=(ACT.Abs_reciprocal_sqrt if RSQRT_ON_SCALAR else ACT.Sqrt), scale=1.0 / 128.0, bias=EPS
+            )
+
+        def recip(e):
+            if RSQRT_ON_SCALAR:
+                rs[e] = rts[e]
+                return
+            rs[e] = small.tile([P, 4], F32, name="r", tag="r")
+            nc.vector.reciprocal(out=rs[e][:], in_=rts[e][:])
+
+        def rope(e, gated):
+            tt = e % 2
+            ab = epi.tile([P, 4, 2, P], F32, name="ab", tag="ab")
+            for h in range(3 if gated else 4):
+                nc.vector.scalar_tensor_tensor(
+                    out=ab[:, h, :, :],
+                    in0=acc[e][:, P * h : P * (h + 1)].unsqueeze(1).to_broadcast([P, 2, P]),
+                    scalar=rs[e][:, h : h + 1],
+                    in1=cs[:, tt, :, :],
+                    op0=ALU.mult,
+                    op1=ALU.mult,
+                )
+            abs_[e] = ab
+            if gated:
+                rope_piece(e, 0)
+
+        def rope_piece(e, plane):
+            nc.vector.scalar_tensor_tensor(
+                out=abs_[e][:, 3, plane, :],
+                in0=acc[e][:, P * 3 : P * 4],
+                scalar=rs[e][:, 3:4],
+                in1=cs[:, e % 2, plane, :],
+                op0=ALU.mult,
+                op1=ALU.mult,
+            )
+
+        def add_store(e):
+            n, m = divmod(e, 4)
+            ab = abs_[e]
+            o = epi.tile([P, 4, P], F32, name="o", tag="o", bufs=4)
+            eng = nc.gpsimd if ADD_ON_GPSIMD else nc.vector
+            eng.tensor_tensor(out=o[:, :, 0:64], in0=ab[:, :, 0, 0:64], in1=ab[:, :, 1, 64:128], op=ALU.add)
+            eng.tensor_tensor(out=o[:, :, 64:128], in0=ab[:, :, 0, 64:128], in1=ab[:, :, 1, 0:64], op=ALU.add)
+            b, t0, h0 = m // 2, P * (m % 2), 4 * (n % 4)
+            nc.sync.dma_start(
+                out=outs[n // 4][b, h0 : h0 + 4, t0 : t0 + P, :].rearrange("h t d -> t h d"),
+                in_=o[:],
+            )
+
+        for k in range(N_TILES + 6):
+            if 1 <= k <= 4:
+                load_w(("pair", 1, k - 1), k - 1, 1024, 1024)
+            if 5 <= k <= 8:
+                load_w(("pair", 2, k - 5), k - 5, 2048, 1024)
+            if 13 <= k <= 16:
+                load_w(("pair", 3, k - 13), k - 13, 3072, 1024)
+            if k < 4:
+                x_transpose(k)
+            pass_through(k + 1)
+            if 1 <= k <= N_TILES:
+                quantize(k - 1)
+                passes(k - 1)
+            if k < N_TILES:
+                if not PT_ON_VECTOR:
+                    pt_evacuate(k)
+                interleave(k, False)
+            if k < 4:
+                x_copy(k, 0, nc.scalar.copy)
+            if k == 2:
+                tables_on_scalar()
+            if k < N_TILES:
+                interleave(k, True)
+            if k < 4:
+                x_copy(k, 1, nc.vector.tensor_copy)
+            if ADD_ON_GPSIMD:
+                if 0 <= k - 6 < N_TILES:
+                    rope_piece(k - 6, 1)
+                    add_store(k - 6)
+                if 0 <= k - 5 < N_TILES:
+                    recip(k - 5)
+            else:
+                if 0 <= k - 5 < N_TILES:
+                    recip(k - 5)
+                if 0 <= k - 6 < N_TILES:
+                    add_store(k - 6)
+            if 0 <= k - 4 < N_TILES:
+                stats(k - 4)
+            if k < N_TILES and PT_ON_VECTOR:
+                pt_evacuate(k)
+            if 0 <= k - 5 < N_TILES:
+                rope(k - 5, ADD_ON_GPSIMD)
+            if k < 4:
+                x_quant(k)

@@ -17,15 +17,13 @@ ACT = mybir.ActivationFunctionType
 
 P = 128
 EPS = 1e-6
-N_TILES = 32
-V_HEAD = 256
-V_STEADY = 80
-V_LAST = 80
-ADD_ON_GPSIMD = True
-PT_COLS = 192
-PT_FIRST = 5
-PT_ON_VECTOR = False
-RSQRT_ON_SCALAR = True
+HEADS = 32
+GROUPS = (256, 256, 512, 1024, 1024, 1024)
+G_COLS = 160
+V_COLS = 192
+V_HEAD = (256, 256, 128, 64, 64, 64)
+LOAD_ORDER = "g0 x0 x1 x2 x3 g1 g2"
+EV_ON_VECTOR = 0
 
 
 def tile_attn_pa_kernel(tc, x, W_qk, out_0, out_1):
@@ -36,47 +34,51 @@ def tile_attn_pa_kernel(tc, x, W_qk, out_0, out_1):
     with ExitStack() as ctx:
         const = ctx.enter_context(tc.tile_pool(name="const", bufs=1))
         xpool = ctx.enter_context(tc.tile_pool(name="xpool", bufs=1))
-        rawp = ctx.enter_context(tc.tile_pool(name="rawp", bufs=8))
-        grp = ctx.enter_context(tc.tile_pool(name="grp", bufs=3))
-        wqp = ctx.enter_context(tc.tile_pool(name="wqp", bufs=5))
+        rawp = ctx.enter_context(tc.tile_pool(name="rawp", bufs=1))
+        grp = ctx.enter_context(tc.tile_pool(name="grp", bufs=2))
+        wqp = ctx.enter_context(tc.tile_pool(name="wqp", bufs=6))
         small = ctx.enter_context(tc.tile_pool(name="small", bufs=4))
         epi = ctx.enter_context(tc.tile_pool(name="epi", bufs=3))
-        psum = ctx.enter_context(tc.psum_pool(name="psum", bufs=6))
+        psum = ctx.enter_context(tc.psum_pool(name="psum", bufs=2))
         ctx.enter_context(tc.manual_schedule())
 
-        xraw = []
-        raw = {}
+        xraw = {}
+        rawg = {}
+        starts = [sum(GROUPS[:i]) for i in range(len(GROUPS))]
 
         def load_x(m):
-            t = xpool.tile([P, 2048], BF16, name="xraw%d" % m)
-            nc.sync.dma_start(out=t[:], in_=xf[P * m : P * (m + 1), :])
-            xraw.append(t)
+            xraw[m] = xpool.tile([P, 2048], BF16, name="xraw%d" % m)
+            nc.sync.dma_start(out=xraw[m][:], in_=xf[P * m : P * (m + 1), :])
 
-        def load_w(key, c, col0, width):
-            t = rawp.tile([P, 4, width], BF16, name="raw", tag="raw")
+        def load_part(gi, c):
+            width = GROUPS[gi]
+            if c == 0:
+                rawg[gi] = rawp.tile([P, 4, 4, width], BF16, name="raw%d" % gi)
             nc.sync.dma_start(
-                out=t[:],
-                in_=W_qk[512 * c : 512 * (c + 1), col0 : col0 + width].rearrange("(p j) w -> p j w", j=4),
+                out=rawg[gi][:, c, :, :],
+                in_=W_qk[512 * c : 512 * (c + 1), starts[gi] : starts[gi] + width].rearrange("(p j) w -> p j w", j=4),
             )
-            raw[key] = t
 
-        for c in range(4):
-            load_w((0, c), c, 0, 512)
-            load_x(c)
-        for c in range(4):
-            load_w((1, c), c, 512, 512)
+        def load_group(gi):
+            for c in range(4):
+                load_part(gi, c)
 
-        def raw_of(k):
-            n, c = divmod(k, 4)
-            if n < 2:
-                return raw[(n, c)], 0
-            return raw[("pair", n // 2, c)], 512 * (n % 2)
+        def raw_of(g):
+            col = P * g
+            gi = max(i for i in range(len(GROUPS)) if starts[i] <= col)
+            return rawg[gi], col - starts[gi]
+
+        for item in LOAD_ORDER.split():
+            if item.startswith("g"):
+                load_group(int(item[1:]))
+            else:
+                load_x(int(item[1:]))
+        later = {2 + c: (3, c) for c in range(4)}
+        later.update({9 + c: (4, c) for c in range(4)})
+        later.update({17 + c: (5, c) for c in range(4)})
 
         ident = const.tile([P, P], F32, name="ident")
         make_identity(nc, ident[:])
-        identb = const.tile([P, P], BF16, name="identb")
-        if PT_COLS:
-            nc.vector.tensor_copy(out=identb[:], in_=ident[:])
         pcol = const.tile([P, 2], F32, name="pcol")
         nc.gpsimd.iota(pcol[:], pattern=[[P, 2]], base=0, channel_multiplier=1, allow_small_or_imprecise_dtypes=True)
         one = const.tile([P, 1], F32, name="one")
@@ -106,217 +108,177 @@ def tile_attn_pa_kernel(tc, x, W_qk, out_0, out_1):
         gm = const.tile([P, 512], F32, name="gm")
         nc.vector.scalar_tensor_tensor(out=gm[:], in0=phf, scalar=0.5, in1=phf, op0=ALU.is_gt, op1=ALU.subtract)
         cs = const.tile([P, 2, 2, P], F32, name="cs")
+        nc.scalar.activation(out=cs[:].rearrange("p a b c -> p (a b c)"), in_=gm[:], func=ACT.Sin, scale=-2.0 * math.pi)
+        swap = const.tile([P, P], F32, name="swap")
+        nc.vector.tensor_copy(out=swap[:, 0:64], in_=ident[:, 64:128])
+        nc.vector.tensor_copy(out=swap[:, 64:128], in_=ident[:, 0:64])
+        tabp = psum.tile([P, 2, 2, P], F32, name="tabp", tag="aux")
+        for plane in range(2):
+            for tt in range(2):
+                nc.tensor.transpose(out=tabp[:, plane, tt, :], in_=cs[:, tt, plane, :], identity=ident[:])
+        tab = const.tile([P, 2, 256], F32, name="tab")
+        nc.vector.tensor_copy(out=tab[:].rearrange("p a t -> p (a t)"), in_=tabp[:].rearrange("p a b c -> p (a b c)"))
 
-        def tables_on_scalar():
-            nc.scalar.activation(out=cs[:].rearrange("p a b c -> p (a b c)"), in_=gm[:], func=ACT.Sin, scale=-2.0 * math.pi)
-            nc.scalar.activation(out=warm[:], in_=one[:], func=(ACT.Abs_reciprocal_sqrt if RSQRT_ON_SCALAR else ACT.Sqrt))
-
-        xq, xs, gxs = [], [], {}
+        gx = xpool.tile([P, 4, 512, 4], BF16, name="gx", align_bytes=64)
+        gxw = gx[:].rearrange("p c r t -> p (c r t)").bitcast(F32).rearrange("p (c r u) -> p c r u", c=4, u=2)
+        xq, xs, xts = {}, {}, {}
 
         def x_transpose(m):
             words = xraw[m][:].bitcast(F32)
-            banks = []
             for cp in range(2):
-                xt = psum.tile([P, 2, 2, P], F32, name="xt", tag="aux", bufs=2)
+                xt = psum.tile([P, 2, 2, P], F32, name="xt", tag="aux")
                 for cc in range(2):
                     c = 2 * cp + cc
                     for u in range(2):
                         nc.tensor.transpose(out=xt[:, cc, u, :], in_=words[:, 256 * c + u : 256 * (c + 1) : 2], identity=ident[:])
-                banks.append(xt)
-            gx = xpool.tile([P, 4, P, 4], BF16, name="gx", tag="gx", bufs=2, align_bytes=64)
-            gxs[m] = (gx, banks)
+                xts[(m, cp)] = xt
 
         def x_copy(m, cp, eng_copy):
-            gx, banks = gxs[m]
-            gw = gx[:].rearrange("p c r t -> p (c r t)").bitcast(F32).rearrange("p (c r u) -> p c r u", c=4, u=2)
-            eng_copy(out=gw[:, 2 * cp : 2 * cp + 2, :, :], in_=banks[cp][:].rearrange("p c u r -> p c r u"))
+            eng_copy(out=gxw[:, 2 * cp : 2 * cp + 2, P * m : P * (m + 1), :], in_=xts[(m, cp)][:].rearrange("p c u r -> p c r u"))
 
-        def x_quant(m):
-            gx, banks = gxs[m]
-            q = xpool.tile([P, 512], U32, name="xq%d" % m, align_bytes=64)
-            s = xpool.tile([P, 512], U8, name="xs%d" % m, align_bytes=64)
-            nc.vector.quantize_mx(out=q[:].bitcast(FP8X4), scales=s[:], in_=gx[:].rearrange("p c r t -> p (c r t)"))
-            xq.append(q)
-            xs.append(s)
+        def x_quant(c):
+            xq[c] = xpool.tile([P, 512], U32, name="xq%d" % c, align_bytes=64)
+            xs[c] = xpool.tile([P, 512], U8, name="xs%d" % c, align_bytes=64)
+            nc.vector.quantize_mx(out=xq[c][:].bitcast(FP8X4), scales=xs[c][:], in_=gx[:, c, :, :].rearrange("p r t -> p (r t)"))
 
-        grouped, wq, ws, acc = {}, {}, {}, {}
+        grouped, wq, ws, t1s, abs_, rbank, rr, os_ = {}, {}, {}, {}, {}, {}, {}, {}
 
-        def v_cols(k):
-            return V_HEAD if k < 5 else (V_LAST if k >= 28 else V_STEADY)
+        def split(g):
+            v = V_HEAD[g] if g < len(V_HEAD) else V_COLS
+            gc = G_COLS if g >= 1 else 0
+            return {"G": (512 - gc, 512), "V": (512 - gc - v, 512 - gc), "S": (0, 512 - gc - v)}
 
-        def pt_cols(k):
-            return PT_COLS if PT_FIRST <= k < N_TILES else 0
-
-        pts = {}
-
-        def pass_through(k):
-            w = pt_cols(k)
-            if w == 0:
-                return
-            t, off = raw_of(k)
-            pt = psum.tile([P, 256, 4], BF16, name="pt", tag="aux", bufs=2)
-            for w0 in range(0, w, 128):
-                w1 = min(w, w0 + 128)
-                nc.tensor.matmul(
-                    out=pt[:, w0:w1, :],
-                    lhsT=identb[:],
-                    rhs=t[:, :, off + 512 - w + w0 : off + 512 - w + w1].rearrange("p j w -> p w j"),
-                    start=True,
-                    stop=True,
-                )
-            pts[k] = pt
-
-        def pt_evacuate(k):
-            w = pt_cols(k)
-            if w == 0:
-                return
-            if k not in grouped:
-                grouped[k] = grp.tile([P, 512, 4], BF16, name="grouped", tag="grouped", align_bytes=64)
-            if PT_ON_VECTOR:
-                nc.vector.tensor_copy(out=grouped[k][:, 512 - w : 512, :], in_=pts[k][:, 0:w, :])
-            else:
-                nc.scalar.copy(out=grouped[k][:, 512 - w : 512, :], in_=pts[k][:, 0:w, :])
-
-        def interleave(k, on_vector):
-            if k not in grouped:
-                grouped[k] = grp.tile([P, 512, 4], BF16, name="grouped", tag="grouped", align_bytes=64)
-            t, off = raw_of(k)
-            v = v_cols(k)
-            lo, hi = (0, v) if on_vector else (v, 512 - pt_cols(k))
+        def interleave(g, who):
+            if g not in grouped:
+                grouped[g] = grp.tile([P, 4, P, 4], BF16, name="grouped", tag="grouped", align_bytes=64)
+            lo, hi = split(g)[who]
             if hi <= lo:
                 return
-            src = t[:, :, off + lo : off + hi].rearrange("p j w -> p w j")
-            if on_vector:
-                nc.vector.tensor_copy(out=grouped[k][:, lo:hi, :], in_=src)
-            else:
-                nc.scalar.copy(out=grouped[k][:, lo:hi, :], in_=src)
+            t, off = raw_of(g)
+            pieces = []
+            pos = lo
+            while pos < hi:
+                c, w = divmod(pos, P)
+                if w == 0 and hi - pos >= P:
+                    n = (hi - pos) // P
+                    pieces.append((c, n, 0, P))
+                    pos += n * P
+                else:
+                    n = min(P - w, hi - pos)
+                    pieces.append((c, 1, w, n))
+                    pos += n
+            for c, nc_, w, n in pieces:
+                src = t[:, c : c + nc_, :, off + w : off + w + n].rearrange("p c j w -> p c w j")
+                dst = grouped[g][:, c : c + nc_, w : w + n, :]
+                if who == "V":
+                    nc.vector.tensor_copy(out=dst, in_=src)
+                elif who == "S":
+                    nc.scalar.copy(out=dst, in_=src)
+                else:
+                    nc.gpsimd.tensor_scalar(out=dst, in0=src, scalar1=1.0, scalar2=0.0, op0=ALU.mult, op1=ALU.add)
 
-        def quantize(k):
-            wq[k] = wqp.tile([P, 512], U32, name="wq", tag="wq", align_bytes=64)
-            ws[k] = wqp.tile([P, 512], U8, name="ws", tag="ws", align_bytes=64)
-            nc.vector.quantize_mx(out=wq[k][:].bitcast(FP8X4), scales=ws[k][:], in_=grouped[k][:].rearrange("p w j -> p (w j)"))
+        def quantize(g):
+            wq[g] = wqp.tile([P, 512], U32, name="wq", tag="wq", align_bytes=64)
+            ws[g] = wqp.tile([P, 512], U8, name="ws", tag="ws", align_bytes=64)
+            nc.vector.quantize_mx(out=wq[g][:].bitcast(FP8X4), scales=ws[g][:], in_=grouped[g][:].rearrange("p c w j -> p (c w j)"))
 
-        def one_pass(k, m):
-            n, c = divmod(k, 4)
-            e = 4 * n + m
-            if c == 0:
-                acc[e] = psum.tile([P, 512], F32, name="acc", tag="acc")
-            nc.tensor.matmul_mx(
-                out=acc[e][:],
-                lhsT=xq[m][:, P * c : P * (c + 1)].bitcast(FP8X4),
-                lhsT_scale=xs[m][:, P * c : P * (c + 1)],
-                rhs=wq[k][:].bitcast(FP8X4),
-                rhs_scale=ws[k][:],
-                start=(c == 0),
-                stop=(c == 3),
-            )
-
-        def passes(j):
-            c = j % 4
-            for m in range(c):
-                one_pass(j, m)
-            for cc in range(c + 1):
-                one_pass(j - c + cc, c)
-
-        rts, rs, abs_ = {}, {}, {}
-
-        def stats(e):
-            ss = small.tile([P, 4], F32, name="ss", tag="ss")
-            for h in range(4):
-                junk = small.tile([P, P], BF16, name="junk", tag="junk", bufs=2)
-                nc.scalar.activation(out=junk[:], in_=acc[e][:, P * h : P * (h + 1)], func=ACT.Square, accum_out=ss[:, h : h + 1])
-            rts[e] = small.tile([P, 4], F32, name="rt", tag="rt")
-            nc.scalar.activation(
-                out=rts[e][:], in_=ss[:], func=(ACT.Abs_reciprocal_sqrt if RSQRT_ON_SCALAR else ACT.Sqrt), scale=1.0 / 128.0, bias=EPS
-            )
-
-        def recip(e):
-            if RSQRT_ON_SCALAR:
-                rs[e] = rts[e]
-                return
-            rs[e] = small.tile([P, 4], F32, name="r", tag="r")
-            nc.vector.reciprocal(out=rs[e][:], in_=rts[e][:])
-
-        def rope(e, gated):
-            tt = e % 2
-            ab = epi.tile([P, 4, 2, P], F32, name="ab", tag="ab")
-            for h in range(3 if gated else 4):
-                nc.vector.scalar_tensor_tensor(
-                    out=ab[:, h, :, :],
-                    in0=acc[e][:, P * h : P * (h + 1)].unsqueeze(1).to_broadcast([P, 2, P]),
-                    scalar=rs[e][:, h : h + 1],
-                    in1=cs[:, tt, :, :],
-                    op0=ALU.mult,
-                    op1=ALU.mult,
+        def passes(g):
+            t1s[g] = psum.tile([P, 512], F32, name="t1", tag="t1", bufs=3)
+            for c in range(4):
+                nc.tensor.matmul_mx(
+                    out=t1s[g][:],
+                    lhsT=wq[g][:, P * c : P * (c + 1)].bitcast(FP8X4),
+                    lhsT_scale=ws[g][:, P * c : P * (c + 1)],
+                    rhs=xq[c][:].bitcast(FP8X4),
+                    rhs_scale=xs[c][:],
+                    start=(c == 0),
+                    stop=(c == 3),
                 )
-            abs_[e] = ab
-            if gated:
-                rope_piece(e, 0)
 
-        def rope_piece(e, plane):
-            nc.vector.scalar_tensor_tensor(
-                out=abs_[e][:, 3, plane, :],
-                in0=acc[e][:, P * 3 : P * 4],
-                scalar=rs[e][:, 3:4],
-                in1=cs[:, e % 2, plane, :],
-                op0=ALU.mult,
-                op1=ALU.mult,
+        def products(g):
+            abs_[g] = epi.tile([P, 2, 2, 256], F32, name="ab", tag="ab")
+            nc.vector.tensor_tensor(
+                out=abs_[g][:],
+                in0=t1s[g][:].rearrange("p (b t) -> p b t", b=2).unsqueeze(1).to_broadcast([P, 2, 2, 256]),
+                in1=tab[:].unsqueeze(2).to_broadcast([P, 2, 2, 256]),
+                op=ALU.mult,
             )
 
-        def add_store(e):
-            n, m = divmod(e, 4)
-            ab = abs_[e]
-            o = epi.tile([P, 4, P], F32, name="o", tag="o", bufs=4)
-            eng = nc.gpsimd if ADD_ON_GPSIMD else nc.vector
-            eng.tensor_tensor(out=o[:, :, 0:64], in0=ab[:, :, 0, 0:64], in1=ab[:, :, 1, 64:128], op=ALU.add)
-            eng.tensor_tensor(out=o[:, :, 64:128], in0=ab[:, :, 0, 64:128], in1=ab[:, :, 1, 0:64], op=ALU.add)
-            b, t0, h0 = m // 2, P * (m % 2), 4 * (n % 4)
-            nc.sync.dma_start(
-                out=outs[n // 4][b, h0 : h0 + 4, t0 : t0 + P, :].rearrange("h t d -> t h d"),
-                in_=o[:],
-            )
+        def turn_and_add(g):
+            rbank[g] = psum.tile([P, 4, P], F32, name="rb", tag="rb", bufs=3)
+            ab = abs_[g][:].rearrange("p a b t -> p a (b t)")
+            for m in range(4):
+                nc.tensor.matmul(out=rbank[g][:, m, :], lhsT=ab[:, 0, P * m : P * (m + 1)], rhs=ident[:], start=True, stop=False, is_transpose=True)
+                nc.tensor.matmul(out=rbank[g][:, m, :], lhsT=ab[:, 1, P * m : P * (m + 1)], rhs=swap[:], start=False, stop=True, is_transpose=True)
 
-        for k in range(N_TILES + 6):
-            if 1 <= k <= 4:
-                load_w(("pair", 1, k - 1), k - 1, 1024, 1024)
-            if 5 <= k <= 8:
-                load_w(("pair", 2, k - 5), k - 5, 2048, 1024)
-            if 13 <= k <= 16:
-                load_w(("pair", 3, k - 13), k - 13, 3072, 1024)
+        sss = {}
+
+        def squares(g):
+            ss = small.tile([P, 4], F32, name="ss", tag="ss")
+            sss[g] = ss
+            for m in range(4):
+                junk = small.tile([P, P], BF16, name="junk", tag="junk", bufs=2)
+                nc.scalar.activation(out=junk[:], in_=rbank[g][:, m, :], func=ACT.Square, accum_out=ss[:, m : m + 1])
+
+        def rsqrt(g):
+            rr[g] = small.tile([P, 4], F32, name="rr", tag="rr")
+            nc.scalar.activation(out=rr[g][:], in_=sss[g][:], func=ACT.Abs_reciprocal_sqrt, scale=1.0 / 128.0, bias=EPS)
+
+        def evacuate(g, on_vector):
+            if g not in os_:
+                os_[g] = epi.tile([P, 4, P], F32, name="o", tag="o", bufs=4)
+            for m in range(4):
+                if (m >= 4 - EV_ON_VECTOR) != on_vector:
+                    continue
+                if on_vector:
+                    nc.vector.tensor_scalar(out=os_[g][:, m, :], in0=rbank[g][:, m, :], scalar1=rr[g][:, m : m + 1], scalar2=None, op0=ALU.mult)
+                else:
+                    nc.scalar.activation(out=os_[g][:, m, :], in_=rbank[g][:, m, :], func=ACT.Copy, scale=rr[g][:, m : m + 1])
+
+        def store(g):
+            for b in range(2):
+                nc.sync.dma_start(
+                    out=outs[g // 16][b, g % 16, :, :].rearrange("(tt p) d -> p tt d", p=P),
+                    in_=os_[g][:, 2 * b : 2 * b + 2, :],
+                )
+
+        def t_mm(g):
+            return max(g + 1, 4 + g // 2)
+
+        def due(k, lag):
+            return [g for g in range(HEADS) if t_mm(g) + lag == k]
+
+        for k in range(HEADS + 5):
+            if k in later:
+                load_part(later[k][0], later[k][1])
             if k < 4:
                 x_transpose(k)
-            pass_through(k + 1)
-            if 1 <= k <= N_TILES:
-                quantize(k - 1)
-                passes(k - 1)
-            if k < N_TILES:
-                if not PT_ON_VECTOR:
-                    pt_evacuate(k)
-                interleave(k, False)
+            for g in due(k, 2):
+                turn_and_add(g)
+            if k < HEADS:
+                interleave(k, "V")
+                interleave(k, "S")
             if k < 4:
                 x_copy(k, 0, nc.scalar.copy)
-            if k == 2:
-                tables_on_scalar()
-            if k < N_TILES:
-                interleave(k, True)
-            if k < 4:
                 x_copy(k, 1, nc.vector.tensor_copy)
-            if ADD_ON_GPSIMD:
-                if 0 <= k - 6 < N_TILES:
-                    rope_piece(k - 6, 1)
-                    add_store(k - 6)
-                if 0 <= k - 5 < N_TILES:
-                    recip(k - 5)
-            else:
-                if 0 <= k - 5 < N_TILES:
-                    recip(k - 5)
-                if 0 <= k - 6 < N_TILES:
-                    add_store(k - 6)
-            if 0 <= k - 4 < N_TILES:
-                stats(k - 4)
-            if k < N_TILES and PT_ON_VECTOR:
-                pt_evacuate(k)
-            if 0 <= k - 5 < N_TILES:
-                rope(k - 5, ADD_ON_GPSIMD)
-            if k < 4:
-                x_quant(k)
+            if k == 3:
+                for c in range(4):
+                    x_quant(c)
+            if 1 <= k <= HEADS:
+                quantize(k - 1)
+            if k + 1 < HEADS:
+                interleave(k + 1, "G")
+            for g in due(k, 0):
+                passes(g)
+            for g in due(k, 1):
+                products(g)
+            d2, d3 = due(k, 2), due(k, 3)
+            for i in range(max(len(d2), len(d3))):
+                if i < len(d2):
+                    squares(d2[i])
+                if i < len(d3):
+                    evacuate(d3[i], False)
+                    evacuate(d3[i], True)
+                    store(d3[i])
+                if i < len(d2):
+                    rsqrt(d2[i])

@@ -19,10 +19,13 @@ P = 128
 EPS = 1e-6
 HEADS = 32
 GROUPS = (256, 256, 512, 1024, 1024, 1024)
-G_COLS = 160
-V_COLS = 192
-V_HEAD = (256, 256, 128, 64, 64, 64)
+G_COLS = 256
+V_COLS = 0
+V_HEAD = (256, 256, 64, 0, 0, 0)
 LOAD_ORDER = "g0 x0 x1 x2 x3 g1 g2"
+EV_WIDE = True
+PT_PASS = 1
+PT_FIRST = 6
 EV_ON_VECTOR = 0
 
 
@@ -109,6 +112,9 @@ def tile_attn_pa_kernel(tc, x, W_qk, out_0, out_1):
         nc.vector.scalar_tensor_tensor(out=gm[:], in0=phf, scalar=0.5, in1=phf, op0=ALU.is_gt, op1=ALU.subtract)
         cs = const.tile([P, 2, 2, P], F32, name="cs")
         nc.scalar.activation(out=cs[:].rearrange("p a b c -> p (a b c)"), in_=gm[:], func=ACT.Sin, scale=-2.0 * math.pi)
+        identb = const.tile([P, P], BF16, name="identb")
+        if PT_PASS:
+            nc.vector.tensor_copy(out=identb[:], in_=ident[:])
         swap = const.tile([P, P], F32, name="swap")
         nc.vector.tensor_copy(out=swap[:, 0:64], in_=ident[:, 64:128])
         nc.vector.tensor_copy(out=swap[:, 64:128], in_=ident[:, 0:64])
@@ -146,7 +152,8 @@ def tile_attn_pa_kernel(tc, x, W_qk, out_0, out_1):
         def split(g):
             v = V_HEAD[g] if g < len(V_HEAD) else V_COLS
             gc = G_COLS if g >= 1 else 0
-            return {"G": (512 - gc, 512), "V": (512 - gc - v, 512 - gc), "S": (0, 512 - gc - v)}
+            pt = P if (PT_PASS and g >= PT_FIRST) else 0
+            return {"G": (512 - gc, 512), "V": (512 - gc - v, 512 - gc), "S": (pt, 512 - gc - v), "PT": (0, pt)}
 
         def interleave(g, who):
             if g not in grouped:
@@ -176,6 +183,22 @@ def tile_attn_pa_kernel(tc, x, W_qk, out_0, out_1):
                     nc.scalar.copy(out=dst, in_=src)
                 else:
                     nc.gpsimd.tensor_scalar(out=dst, in0=src, scalar1=1.0, scalar2=0.0, op0=ALU.mult, op1=ALU.add)
+
+        pts = {}
+
+        def pass_through(g):
+            if g >= HEADS or split(g)["PT"][1] == 0:
+                return
+            t, off = raw_of(g)
+            pts[g] = psum.tile([P, P, 4], BF16, name="pt", tag="aux")
+            nc.tensor.matmul(out=pts[g][:], lhsT=identb[:], rhs=t[:, 0, :, off : off + P].rearrange("p j w -> p w j"), start=True, stop=True)
+
+        def pt_evacuate(g):
+            if split(g)["PT"][1] == 0:
+                return
+            if g not in grouped:
+                grouped[g] = grp.tile([P, 4, P, 4], BF16, name="grouped", tag="grouped", align_bytes=64)
+            nc.scalar.copy(out=grouped[g][:, 0, :, :], in_=pts[g][:])
 
         def quantize(g):
             wq[g] = wqp.tile([P, 512], U32, name="wq", tag="wq", align_bytes=64)
@@ -227,6 +250,10 @@ def tile_attn_pa_kernel(tc, x, W_qk, out_0, out_1):
         def evacuate(g, on_vector):
             if g not in os_:
                 os_[g] = epi.tile([P, 4, P], F32, name="o", tag="o", bufs=4)
+            if EV_WIDE:
+                if on_vector:
+                    nc.vector.tensor_tensor(out=os_[g][:], in0=rbank[g][:], in1=rr[g][:].unsqueeze(2).to_broadcast([P, 4, P]), op=ALU.mult)
+                return
             for m in range(4):
                 if (m >= 4 - EV_ON_VECTOR) != on_vector:
                     continue
@@ -255,8 +282,10 @@ def tile_attn_pa_kernel(tc, x, W_qk, out_0, out_1):
                 x_transpose(k)
             for g in due(k, 2):
                 turn_and_add(g)
+            pass_through(k + 1)
             if k < HEADS:
                 interleave(k, "V")
+                pt_evacuate(k)
                 interleave(k, "S")
             if k < 4:
                 x_copy(k, 0, nc.scalar.copy)
@@ -270,10 +299,10 @@ def tile_attn_pa_kernel(tc, x, W_qk, out_0, out_1):
                 interleave(k + 1, "G")
             for g in due(k, 0):
                 passes(g)
-            for g in due(k, 1):
-                products(g)
-            d2, d3 = due(k, 2), due(k, 3)
-            for i in range(max(len(d2), len(d3))):
+            d1, d2, d3 = due(k, 1), due(k, 2), due(k, 3)
+            for i in range(max(len(d1), len(d2), len(d3))):
+                if i < len(d1):
+                    products(d1[i])
                 if i < len(d2):
                     squares(d2[i])
                 if i < len(d3):

@@ -17,16 +17,16 @@ ACT = mybir.ActivationFunctionType
 
 P = 128
 EPS = 1e-6
-HEADS = 32
-GROUPS = (256, 256, 512, 1024, 1024, 1024)
-G_COLS = 256
-V_COLS = 0
-V_HEAD = (256, 256, 64, 0, 0, 0)
-LOAD_ORDER = "g0 x0 x1 x2 x3 g1 g2"
-EV_WIDE = True
-PT_PASS = 1
-PT_FIRST = 6
-EV_ON_VECTOR = 0
+N_TILES = 32
+V_HEAD = 256
+V_STEADY = 0
+V_LAST = 0
+ADD_ON_GPSIMD = True
+ADD_HALF = False
+PT_COLS = 240
+PT_FIRST = 5
+PT_ON_VECTOR = True
+RSQRT_ON_SCALAR = True
 
 
 def tile_attn_pa_kernel(tc, x, W_qk, out_0, out_1):
@@ -37,51 +37,47 @@ def tile_attn_pa_kernel(tc, x, W_qk, out_0, out_1):
     with ExitStack() as ctx:
         const = ctx.enter_context(tc.tile_pool(name="const", bufs=1))
         xpool = ctx.enter_context(tc.tile_pool(name="xpool", bufs=1))
-        rawp = ctx.enter_context(tc.tile_pool(name="rawp", bufs=1))
-        grp = ctx.enter_context(tc.tile_pool(name="grp", bufs=2))
-        wqp = ctx.enter_context(tc.tile_pool(name="wqp", bufs=6))
+        rawp = ctx.enter_context(tc.tile_pool(name="rawp", bufs=8))
+        grp = ctx.enter_context(tc.tile_pool(name="grp", bufs=3))
+        wqp = ctx.enter_context(tc.tile_pool(name="wqp", bufs=5))
         small = ctx.enter_context(tc.tile_pool(name="small", bufs=4))
         epi = ctx.enter_context(tc.tile_pool(name="epi", bufs=3))
-        psum = ctx.enter_context(tc.psum_pool(name="psum", bufs=2))
+        psum = ctx.enter_context(tc.psum_pool(name="psum", bufs=6))
         ctx.enter_context(tc.manual_schedule())
 
-        xraw = {}
-        rawg = {}
-        starts = [sum(GROUPS[:i]) for i in range(len(GROUPS))]
+        xraw = []
+        raw = {}
 
         def load_x(m):
-            xraw[m] = xpool.tile([P, 2048], BF16, name="xraw%d" % m)
-            nc.sync.dma_start(out=xraw[m][:], in_=xf[P * m : P * (m + 1), :])
+            t = xpool.tile([P, 2048], BF16, name="xraw%d" % m)
+            nc.sync.dma_start(out=t[:], in_=xf[P * m : P * (m + 1), :])
+            xraw.append(t)
 
-        def load_part(gi, c):
-            width = GROUPS[gi]
-            if c == 0:
-                rawg[gi] = rawp.tile([P, 4, 4, width], BF16, name="raw%d" % gi)
+        def load_w(key, c, col0, width):
+            t = rawp.tile([P, 4, width], BF16, name="raw", tag="raw")
             nc.sync.dma_start(
-                out=rawg[gi][:, c, :, :],
-                in_=W_qk[512 * c : 512 * (c + 1), starts[gi] : starts[gi] + width].rearrange("(p j) w -> p j w", j=4),
+                out=t[:],
+                in_=W_qk[512 * c : 512 * (c + 1), col0 : col0 + width].rearrange("(p j) w -> p j w", j=4),
             )
+            raw[key] = t
 
-        def load_group(gi):
-            for c in range(4):
-                load_part(gi, c)
+        for c in range(4):
+            load_w((0, c), c, 0, 512)
+            load_x(c)
+        for c in range(4):
+            load_w((1, c), c, 512, 512)
 
-        def raw_of(g):
-            col = P * g
-            gi = max(i for i in range(len(GROUPS)) if starts[i] <= col)
-            return rawg[gi], col - starts[gi]
-
-        for item in LOAD_ORDER.split():
-            if item.startswith("g"):
-                load_group(int(item[1:]))
-            else:
-                load_x(int(item[1:]))
-        later = {2 + c: (3, c) for c in range(4)}
-        later.update({9 + c: (4, c) for c in range(4)})
-        later.update({17 + c: (5, c) for c in range(4)})
+        def raw_of(k):
+            n, c = divmod(k, 4)
+            if n < 2:
+                return raw[(n, c)], 0
+            return raw[("pair", n // 2, c)], 512 * (n % 2)
 
         ident = const.tile([P, P], F32, name="ident")
         make_identity(nc, ident[:])
+        identb = const.tile([P, P], BF16, name="identb")
+        if PT_COLS:
+            nc.vector.tensor_copy(out=identb[:], in_=ident[:])
         pcol = const.tile([P, 2], F32, name="pcol")
         nc.gpsimd.iota(pcol[:], pattern=[[P, 2]], base=0, channel_multiplier=1, allow_small_or_imprecise_dtypes=True)
         one = const.tile([P, 1], F32, name="one")
@@ -111,203 +107,232 @@ def tile_attn_pa_kernel(tc, x, W_qk, out_0, out_1):
         gm = const.tile([P, 512], F32, name="gm")
         nc.vector.scalar_tensor_tensor(out=gm[:], in0=phf, scalar=0.5, in1=phf, op0=ALU.is_gt, op1=ALU.subtract)
         cs = const.tile([P, 2, 2, P], F32, name="cs")
-        nc.scalar.activation(out=cs[:].rearrange("p a b c -> p (a b c)"), in_=gm[:], func=ACT.Sin, scale=-2.0 * math.pi)
-        identb = const.tile([P, P], BF16, name="identb")
-        if PT_PASS:
-            nc.vector.tensor_copy(out=identb[:], in_=ident[:])
-        swap = const.tile([P, P], F32, name="swap")
-        nc.vector.tensor_copy(out=swap[:, 0:64], in_=ident[:, 64:128])
-        nc.vector.tensor_copy(out=swap[:, 64:128], in_=ident[:, 0:64])
-        tabp = psum.tile([P, 2, 2, P], F32, name="tabp", tag="aux")
-        for plane in range(2):
-            for tt in range(2):
-                nc.tensor.transpose(out=tabp[:, plane, tt, :], in_=cs[:, tt, plane, :], identity=ident[:])
-        tab = const.tile([P, 2, 256], F32, name="tab")
-        nc.vector.tensor_copy(out=tab[:].rearrange("p a t -> p (a t)"), in_=tabp[:].rearrange("p a b c -> p (a b c)"))
 
-        gx = xpool.tile([P, 4, 512, 4], BF16, name="gx", align_bytes=64)
-        gxw = gx[:].rearrange("p c r t -> p (c r t)").bitcast(F32).rearrange("p (c r u) -> p c r u", c=4, u=2)
-        xq, xs, xts = {}, {}, {}
+        def tables_on_scalar():
+            nc.scalar.activation(out=cs[:].rearrange("p a b c -> p (a b c)"), in_=gm[:], func=ACT.Sin, scale=-2.0 * math.pi)
+            nc.scalar.activation(out=warm[:], in_=one[:], func=(ACT.Abs_reciprocal_sqrt if RSQRT_ON_SCALAR else ACT.Sqrt))
+
+        xq, xs, gxs = [], [], {}
 
         def x_transpose(m):
             words = xraw[m][:].bitcast(F32)
+            banks = []
             for cp in range(2):
-                xt = psum.tile([P, 2, 2, P], F32, name="xt", tag="aux")
+                xt = psum.tile([P, 2, 2, P], F32, name="xt", tag="aux", bufs=2)
                 for cc in range(2):
                     c = 2 * cp + cc
                     for u in range(2):
                         nc.tensor.transpose(out=xt[:, cc, u, :], in_=words[:, 256 * c + u : 256 * (c + 1) : 2], identity=ident[:])
-                xts[(m, cp)] = xt
+                banks.append(xt)
+            gx = xpool.tile([P, 4, P, 4], BF16, name="gx", tag="gx", bufs=2, align_bytes=64)
+            gxs[m] = (gx, banks)
 
         def x_copy(m, cp, eng_copy):
-            eng_copy(out=gxw[:, 2 * cp : 2 * cp + 2, P * m : P * (m + 1), :], in_=xts[(m, cp)][:].rearrange("p c u r -> p c r u"))
+            gx, banks = gxs[m]
+            gw = gx[:].rearrange("p c r t -> p (c r t)").bitcast(F32).rearrange("p (c r u) -> p c r u", c=4, u=2)
+            eng_copy(out=gw[:, 2 * cp : 2 * cp + 2, :, :], in_=banks[cp][:].rearrange("p c u r -> p c r u"))
 
-        def x_quant(c):
-            xq[c] = xpool.tile([P, 512], U32, name="xq%d" % c, align_bytes=64)
-            xs[c] = xpool.tile([P, 512], U8, name="xs%d" % c, align_bytes=64)
-            nc.vector.quantize_mx(out=xq[c][:].bitcast(FP8X4), scales=xs[c][:], in_=gx[:, c, :, :].rearrange("p r t -> p (r t)"))
+        def x_quant(m):
+            gx, banks = gxs[m]
+            q = xpool.tile([P, 512], U32, name="xq%d" % m, align_bytes=64)
+            s = xpool.tile([P, 512], U8, name="xs%d" % m, align_bytes=64)
+            nc.vector.quantize_mx(out=q[:].bitcast(FP8X4), scales=s[:], in_=gx[:].rearrange("p c r t -> p (c r t)"))
+            xq.append(q)
+            xs.append(s)
 
-        grouped, wq, ws, t1s, abs_, rbank, rr, os_ = {}, {}, {}, {}, {}, {}, {}, {}
+        grouped, wq, ws, acc = {}, {}, {}, {}
 
-        def split(g):
-            v = V_HEAD[g] if g < len(V_HEAD) else V_COLS
-            gc = G_COLS if g >= 1 else 0
-            pt = P if (PT_PASS and g >= PT_FIRST) else 0
-            return {"G": (512 - gc, 512), "V": (512 - gc - v, 512 - gc), "S": (pt, 512 - gc - v), "PT": (0, pt)}
+        def v_cols(k):
+            return V_HEAD if k < 5 else (V_LAST if k >= 28 else V_STEADY)
 
-        def interleave(g, who):
-            if g not in grouped:
-                grouped[g] = grp.tile([P, 4, P, 4], BF16, name="grouped", tag="grouped", align_bytes=64)
-            lo, hi = split(g)[who]
-            if hi <= lo:
-                return
-            t, off = raw_of(g)
-            pieces = []
-            pos = lo
-            while pos < hi:
-                c, w = divmod(pos, P)
-                if w == 0 and hi - pos >= P:
-                    n = (hi - pos) // P
-                    pieces.append((c, n, 0, P))
-                    pos += n * P
-                else:
-                    n = min(P - w, hi - pos)
-                    pieces.append((c, 1, w, n))
-                    pos += n
-            for c, nc_, w, n in pieces:
-                src = t[:, c : c + nc_, :, off + w : off + w + n].rearrange("p c j w -> p c w j")
-                dst = grouped[g][:, c : c + nc_, w : w + n, :]
-                if who == "V":
-                    nc.vector.tensor_copy(out=dst, in_=src)
-                elif who == "S":
-                    nc.scalar.copy(out=dst, in_=src)
-                else:
-                    nc.gpsimd.tensor_scalar(out=dst, in0=src, scalar1=1.0, scalar2=0.0, op0=ALU.mult, op1=ALU.add)
+        def pt_cols(k):
+            return PT_COLS if PT_FIRST <= k < N_TILES else 0
 
         pts = {}
 
-        def pass_through(g):
-            if g >= HEADS or split(g)["PT"][1] == 0:
+        def pass_through(k):
+            w = pt_cols(k)
+            if w == 0:
                 return
-            t, off = raw_of(g)
-            pts[g] = psum.tile([P, P, 4], BF16, name="pt", tag="aux")
-            nc.tensor.matmul(out=pts[g][:], lhsT=identb[:], rhs=t[:, 0, :, off : off + P].rearrange("p j w -> p w j"), start=True, stop=True)
-
-        def pt_evacuate(g):
-            if split(g)["PT"][1] == 0:
-                return
-            if g not in grouped:
-                grouped[g] = grp.tile([P, 4, P, 4], BF16, name="grouped", tag="grouped", align_bytes=64)
-            nc.scalar.copy(out=grouped[g][:, 0, :, :], in_=pts[g][:])
-
-        def quantize(g):
-            wq[g] = wqp.tile([P, 512], U32, name="wq", tag="wq", align_bytes=64)
-            ws[g] = wqp.tile([P, 512], U8, name="ws", tag="ws", align_bytes=64)
-            nc.vector.quantize_mx(out=wq[g][:].bitcast(FP8X4), scales=ws[g][:], in_=grouped[g][:].rearrange("p c w j -> p (c w j)"))
-
-        def passes(g):
-            t1s[g] = psum.tile([P, 512], F32, name="t1", tag="t1", bufs=3)
-            for c in range(4):
-                nc.tensor.matmul_mx(
-                    out=t1s[g][:],
-                    lhsT=wq[g][:, P * c : P * (c + 1)].bitcast(FP8X4),
-                    lhsT_scale=ws[g][:, P * c : P * (c + 1)],
-                    rhs=xq[c][:].bitcast(FP8X4),
-                    rhs_scale=xs[c][:],
-                    start=(c == 0),
-                    stop=(c == 3),
+            t, off = raw_of(k)
+            pt = psum.tile([P, 256, 4], BF16, name="pt", tag="aux", bufs=2)
+            for w0 in range(0, w, 128):
+                w1 = min(w, w0 + 128)
+                nc.tensor.matmul(
+                    out=pt[:, w0:w1, :],
+                    lhsT=identb[:],
+                    rhs=t[:, :, off + 512 - w + w0 : off + 512 - w + w1].rearrange("p j w -> p w j"),
+                    start=True,
+                    stop=True,
                 )
+            pts[k] = pt
 
-        def products(g):
-            abs_[g] = epi.tile([P, 2, 2, 256], F32, name="ab", tag="ab")
-            nc.vector.tensor_tensor(
-                out=abs_[g][:],
-                in0=t1s[g][:].rearrange("p (b t) -> p b t", b=2).unsqueeze(1).to_broadcast([P, 2, 2, 256]),
-                in1=tab[:].unsqueeze(2).to_broadcast([P, 2, 2, 256]),
-                op=ALU.mult,
+        def pt_evacuate(k):
+            w = pt_cols(k)
+            if w == 0:
+                return
+            if k not in grouped:
+                grouped[k] = grp.tile([P, 512, 4], BF16, name="grouped", tag="grouped", align_bytes=64)
+            if PT_ON_VECTOR:
+                nc.vector.tensor_copy(out=grouped[k][:, 512 - w : 512, :], in_=pts[k][:, 0:w, :])
+            else:
+                nc.scalar.copy(out=grouped[k][:, 512 - w : 512, :], in_=pts[k][:, 0:w, :])
+
+        def interleave(k, on_vector):
+            if k not in grouped:
+                grouped[k] = grp.tile([P, 512, 4], BF16, name="grouped", tag="grouped", align_bytes=64)
+            t, off = raw_of(k)
+            v = v_cols(k)
+            lo, hi = (0, v) if on_vector else (v, 512 - pt_cols(k))
+            if hi <= lo:
+                return
+            src = t[:, :, off + lo : off + hi].rearrange("p j w -> p w j")
+            if on_vector:
+                nc.vector.tensor_copy(out=grouped[k][:, lo:hi, :], in_=src)
+            else:
+                nc.scalar.copy(out=grouped[k][:, lo:hi, :], in_=src)
+
+        def quantize(k):
+            wq[k] = wqp.tile([P, 512], U32, name="wq", tag="wq", align_bytes=64)
+            ws[k] = wqp.tile([P, 512], U8, name="ws", tag="ws", align_bytes=64)
+            nc.vector.quantize_mx(out=wq[k][:].bitcast(FP8X4), scales=ws[k][:], in_=grouped[k][:].rearrange("p w j -> p (w j)"))
+
+        def one_pass(k, m):
+            n, c = divmod(k, 4)
+            e = 4 * n + m
+            if c == 0:
+                acc[e] = psum.tile([P, 512], F32, name="acc", tag="acc")
+            nc.tensor.matmul_mx(
+                out=acc[e][:],
+                lhsT=xq[m][:, P * c : P * (c + 1)].bitcast(FP8X4),
+                lhsT_scale=xs[m][:, P * c : P * (c + 1)],
+                rhs=wq[k][:].bitcast(FP8X4),
+                rhs_scale=ws[k][:],
+                start=(c == 0),
+                stop=(c == 3),
             )
 
-        def turn_and_add(g):
-            rbank[g] = psum.tile([P, 4, P], F32, name="rb", tag="rb", bufs=3)
-            ab = abs_[g][:].rearrange("p a b t -> p a (b t)")
-            for m in range(4):
-                nc.tensor.matmul(out=rbank[g][:, m, :], lhsT=ab[:, 0, P * m : P * (m + 1)], rhs=ident[:], start=True, stop=False, is_transpose=True)
-                nc.tensor.matmul(out=rbank[g][:, m, :], lhsT=ab[:, 1, P * m : P * (m + 1)], rhs=swap[:], start=False, stop=True, is_transpose=True)
+        def passes(j):
+            c = j % 4
+            for m in range(c):
+                one_pass(j, m)
+            for cc in range(c + 1):
+                one_pass(j - c + cc, c)
 
-        sss = {}
+        rts, rs, abs_ = {}, {}, {}
 
-        def squares(g):
+        def stats(e):
             ss = small.tile([P, 4], F32, name="ss", tag="ss")
-            sss[g] = ss
-            for m in range(4):
+            for h in range(4):
                 junk = small.tile([P, P], BF16, name="junk", tag="junk", bufs=2)
-                nc.scalar.activation(out=junk[:], in_=rbank[g][:, m, :], func=ACT.Square, accum_out=ss[:, m : m + 1])
+                nc.scalar.activation(out=junk[:], in_=acc[e][:, P * h : P * (h + 1)], func=ACT.Square, accum_out=ss[:, h : h + 1])
+            rts[e] = small.tile([P, 4], F32, name="rt", tag="rt")
+            nc.scalar.activation(
+                out=rts[e][:], in_=ss[:], func=(ACT.Abs_reciprocal_sqrt if RSQRT_ON_SCALAR else ACT.Sqrt), scale=1.0 / 128.0, bias=EPS
+            )
 
-        def rsqrt(g):
-            rr[g] = small.tile([P, 4], F32, name="rr", tag="rr")
-            nc.scalar.activation(out=rr[g][:], in_=sss[g][:], func=ACT.Abs_reciprocal_sqrt, scale=1.0 / 128.0, bias=EPS)
-
-        def evacuate(g, on_vector):
-            if g not in os_:
-                os_[g] = epi.tile([P, 4, P], F32, name="o", tag="o", bufs=4)
-            if EV_WIDE:
-                if on_vector:
-                    nc.vector.tensor_tensor(out=os_[g][:], in0=rbank[g][:], in1=rr[g][:].unsqueeze(2).to_broadcast([P, 4, P]), op=ALU.mult)
+        def recip(e):
+            if RSQRT_ON_SCALAR:
+                rs[e] = rts[e]
                 return
-            for m in range(4):
-                if (m >= 4 - EV_ON_VECTOR) != on_vector:
-                    continue
-                if on_vector:
-                    nc.vector.tensor_scalar(out=os_[g][:, m, :], in0=rbank[g][:, m, :], scalar1=rr[g][:, m : m + 1], scalar2=None, op0=ALU.mult)
-                else:
-                    nc.scalar.activation(out=os_[g][:, m, :], in_=rbank[g][:, m, :], func=ACT.Copy, scale=rr[g][:, m : m + 1])
+            rs[e] = small.tile([P, 4], F32, name="r", tag="r")
+            nc.vector.reciprocal(out=rs[e][:], in_=rts[e][:])
 
-        def store(g):
-            for b in range(2):
-                nc.sync.dma_start(
-                    out=outs[g // 16][b, g % 16, :, :].rearrange("(tt p) d -> p tt d", p=P),
-                    in_=os_[g][:, 2 * b : 2 * b + 2, :],
+        def rope(e, gated):
+            tt = e % 2
+            ab = epi.tile([P, 4, 2, P], F32, name="ab", tag="ab")
+            for h in range(3 if gated else 4):
+                nc.vector.scalar_tensor_tensor(
+                    out=ab[:, h, :, :],
+                    in0=acc[e][:, P * h : P * (h + 1)].unsqueeze(1).to_broadcast([P, 2, P]),
+                    scalar=rs[e][:, h : h + 1],
+                    in1=cs[:, tt, :, :],
+                    op0=ALU.mult,
+                    op1=ALU.mult,
                 )
+            abs_[e] = ab
+            if gated:
+                rope_piece(e, 0, 0, P)
+                if ADD_HALF:
+                    rope_piece(e, 1, 64, P)
 
-        def t_mm(g):
-            return max(g + 1, 4 + g // 2)
+        def rope_piece(e, plane, lo, hi):
+            nc.vector.scalar_tensor_tensor(
+                out=abs_[e][:, 3, plane, lo:hi],
+                in0=acc[e][:, P * 3 + lo : P * 3 + hi],
+                scalar=rs[e][:, 3:4],
+                in1=cs[:, e % 2, plane, lo:hi],
+                op0=ALU.mult,
+                op1=ALU.mult,
+            )
 
-        def due(k, lag):
-            return [g for g in range(HEADS) if t_mm(g) + lag == k]
+        os_ = {}
 
-        for k in range(HEADS + 5):
-            if k in later:
-                load_part(later[k][0], later[k][1])
+        def add_low(e, eng):
+            os_[e] = epi.tile([P, 4, P], F32, name="o", tag="o", bufs=4)
+            ab = abs_[e]
+            eng.tensor_tensor(out=os_[e][:, :, 0:64], in0=ab[:, :, 0, 0:64], in1=ab[:, :, 1, 64:128], op=ALU.add)
+
+        def add_store(e, with_low=True):
+            n, m = divmod(e, 4)
+            ab = abs_[e]
+            eng = nc.gpsimd if ADD_ON_GPSIMD else nc.vector
+            if with_low:
+                add_low(e, eng)
+            o = os_[e]
+            eng.tensor_tensor(out=o[:, :, 64:128], in0=ab[:, :, 0, 64:128], in1=ab[:, :, 1, 0:64], op=ALU.add)
+            b, t0, h0 = m // 2, P * (m % 2), 4 * (n % 4)
+            nc.sync.dma_start(
+                out=outs[n // 4][b, h0 : h0 + 4, t0 : t0 + P, :].rearrange("h t d -> t h d"),
+                in_=o[:],
+            )
+
+        for k in range(N_TILES + 6):
+            if 1 <= k <= 4:
+                load_w(("pair", 1, k - 1), k - 1, 1024, 1024)
+            if 5 <= k <= 8:
+                load_w(("pair", 2, k - 5), k - 5, 2048, 1024)
+            if 13 <= k <= 16:
+                load_w(("pair", 3, k - 13), k - 13, 3072, 1024)
             if k < 4:
                 x_transpose(k)
-            for g in due(k, 2):
-                turn_and_add(g)
             pass_through(k + 1)
-            if k < HEADS:
-                interleave(k, "V")
-                pt_evacuate(k)
-                interleave(k, "S")
+            if 1 <= k <= N_TILES:
+                quantize(k - 1)
+                passes(k - 1)
+            if k < N_TILES:
+                if not PT_ON_VECTOR:
+                    pt_evacuate(k)
+                interleave(k, False)
             if k < 4:
                 x_copy(k, 0, nc.scalar.copy)
+            if k == 2:
+                tables_on_scalar()
+            if k < N_TILES:
+                interleave(k, True)
+            if k < 4:
                 x_copy(k, 1, nc.vector.tensor_copy)
-            if k == 3:
-                for c in range(4):
-                    x_quant(c)
-            if 1 <= k <= HEADS:
-                quantize(k - 1)
-            if k + 1 < HEADS:
-                interleave(k + 1, "G")
-            for g in due(k, 0):
-                passes(g)
-            d1, d2, d3 = due(k, 1), due(k, 2), due(k, 3)
-            for i in range(max(len(d1), len(d2), len(d3))):
-                if i < len(d1):
-                    products(d1[i])
-                if i < len(d2):
-                    squares(d2[i])
-                if i < len(d3):
-                    evacuate(d3[i], False)
-                    evacuate(d3[i], True)
-                    store(d3[i])
-                if i < len(d2):
-                    rsqrt(d2[i])
+            if ADD_ON_GPSIMD:
+                if 0 <= k - 6 < N_TILES:
+                    if ADD_HALF:
+                        add_low(k - 6, nc.vector)
+                        rope_piece(k - 6, 1, 0, 64)
+                        add_store(k - 6, False)
+                    else:
+                        rope_piece(k - 6, 1, 0, P)
+                        add_store(k - 6)
+                if 0 <= k - 5 < N_TILES:
+                    recip(k - 5)
+            else:
+                if 0 <= k - 5 < N_TILES:
+                    recip(k - 5)
+                if 0 <= k - 6 < N_TILES:
+                    add_store(k - 6)
+            if 0 <= k - 4 < N_TILES:
+                stats(k - 4)
+            if k < N_TILES and PT_ON_VECTOR:
+                pt_evacuate(k)
+            if 0 <= k - 5 < N_TILES:
+                rope(k - 5, ADD_ON_GPSIMD)
+            if k < 4:
+                x_quant(k)

@@ -16,17 +16,28 @@ ALU = mybir.AluOpType
 ACT = mybir.ActivationFunctionType
 
 P = 128
+HALF = 64
+PACK = 4
+K_PASS = P * PACK
+PASSES = 4
+BLOCK = 512
+HEADS_IN_BANK = 4
+TOKEN_TILES = 4
+W_TILES = 32
+BANKS = 32
 EPS = 1e-6
-N_TILES = 32
-V_HEAD = 256
-V_STEADY = 0
-V_LAST = 0
-ADD_ON_GPSIMD = True
-ADD_HALF = False
-PT_COLS = 240
-PT_FIRST = 5
-PT_ON_VECTOR = True
-RSQRT_ON_SCALAR = True
+ROPE_BASE = 10000.0
+
+TENSOR_COLS = 240
+FIRST_TENSOR_TILE = 5
+VECTOR_COLS = 192
+LAST_VECTOR_TILE = 4
+
+SQUARES_LAG = 4
+PRODUCTS_LAG = 5
+ADD_LAG = 6
+
+PAIR_LOAD_STEPS = (1, 9, 17)
 
 
 def tile_attn_pa_kernel(tc, x, W_qk, out_0, out_1):
@@ -49,290 +60,263 @@ def tile_attn_pa_kernel(tc, x, W_qk, out_0, out_1):
         raw = {}
 
         def load_x(m):
-            t = xpool.tile([P, 2048], BF16, name="xraw%d" % m)
-            nc.sync.dma_start(out=t[:], in_=xf[P * m : P * (m + 1), :])
-            xraw.append(t)
+            tokens = xpool.tile([P, 2048], BF16, name="xraw%d" % m)
+            nc.sync.dma_start(out=tokens[:], in_=xf[P * m : P * (m + 1), :])
+            xraw.append(tokens)
 
         def load_w(key, c, col0, width):
-            t = rawp.tile([P, 4, width], BF16, name="raw", tag="raw")
+            rows = rawp.tile([P, PACK, width], BF16, name="raw", tag="raw")
             nc.sync.dma_start(
-                out=t[:],
-                in_=W_qk[512 * c : 512 * (c + 1), col0 : col0 + width].rearrange("(p j) w -> p j w", j=4),
+                out=rows[:],
+                in_=W_qk[K_PASS * c : K_PASS * (c + 1), col0 : col0 + width].rearrange("(p j) w -> p j w", j=PACK),
             )
-            raw[key] = t
+            raw[key] = rows
 
-        for c in range(4):
-            load_w((0, c), c, 0, 512)
+        for c in range(PASSES):
+            load_w((0, c), c, 0, BLOCK)
             load_x(c)
-        for c in range(4):
-            load_w((1, c), c, 512, 512)
+        for c in range(PASSES):
+            load_w((1, c), c, BLOCK, BLOCK)
 
         def raw_of(k):
-            n, c = divmod(k, 4)
+            n, c = divmod(k, PASSES)
             if n < 2:
                 return raw[(n, c)], 0
-            return raw[("pair", n // 2, c)], 512 * (n % 2)
+            return raw[("pair", n // 2, c)], BLOCK * (n % 2)
 
         ident = const.tile([P, P], F32, name="ident")
         make_identity(nc, ident[:])
         identb = const.tile([P, P], BF16, name="identb")
-        if PT_COLS:
-            nc.vector.tensor_copy(out=identb[:], in_=ident[:])
-        pcol = const.tile([P, 2], F32, name="pcol")
-        nc.gpsimd.iota(pcol[:], pattern=[[P, 2]], base=0, channel_multiplier=1, allow_small_or_imprecise_dtypes=True)
+        nc.vector.tensor_copy(out=identb[:], in_=ident[:])
+
+        pos = const.tile([P, 2], F32, name="pcol")
+        nc.gpsimd.iota(pos[:], pattern=[[P, 2]], base=0, channel_multiplier=1, allow_small_or_imprecise_dtypes=True)
         one = const.tile([P, 1], F32, name="one")
         nc.vector.memset(one[:], 1.0)
         warm = const.tile([P, 1], F32, name="warm")
         nc.scalar.activation(out=warm[:], in_=one[:], func=ACT.Sin)
-        phi = const.tile([P, 64], F32, name="phi")
-        nc.vector.tensor_scalar(out=phi[:, 0:1], in0=one[:], scalar1=1.0 / (2.0 * math.pi), scalar2=None, op0=ALU.mult)
-        ratio = 10000.0 ** (-2.0 / 128.0)
+        freq = const.tile([P, HALF], F32, name="phi")
+        nc.vector.tensor_scalar(out=freq[:, 0:1], in0=one[:], scalar1=1.0 / (2.0 * math.pi), scalar2=None, op0=ALU.mult)
+        ratio = ROPE_BASE ** (-2.0 / P)
         for s in range(6):
             w = 2 ** s
-            nc.vector.tensor_scalar(out=phi[:, w : 2 * w], in0=phi[:, 0:w], scalar1=ratio ** w, scalar2=None, op0=ALU.mult)
-        turns = const.tile([P, 2, 64], F32, name="turns")
-        for tt in range(2):
-            nc.vector.tensor_scalar(out=turns[:, tt, :], in0=phi[:], scalar1=pcol[:, tt : tt + 1], scalar2=None, op0=ALU.mult)
-        tf = turns[:].rearrange("p a c -> p (a c)")
-        ki = const.tile([P, 128], I32, name="ki")
-        nc.vector.tensor_copy(out=ki[:], in_=tf)
-        kf = const.tile([P, 128], F32, name="kf")
-        nc.vector.tensor_copy(out=kf[:], in_=ki[:])
-        fr = const.tile([P, 2, 64], F32, name="fr")
-        nc.vector.tensor_tensor(out=fr[:].rearrange("p a c -> p (a c)"), in0=tf, in1=kf[:], op=ALU.subtract)
-        ph = const.tile([P, 2, 4, 64], F32, name="ph")
-        for blk, off in enumerate((0.25, 0.25, 0.0, 0.5)):
-            nc.vector.tensor_scalar(out=ph[:, :, blk, :], in0=fr[:], scalar1=off, scalar2=None, op0=ALU.add)
-        phf = ph[:].rearrange("p a b c -> p (a b c)")
-        gm = const.tile([P, 512], F32, name="gm")
-        nc.vector.scalar_tensor_tensor(out=gm[:], in0=phf, scalar=0.5, in1=phf, op0=ALU.is_gt, op1=ALU.subtract)
-        cs = const.tile([P, 2, 2, P], F32, name="cs")
+            nc.vector.tensor_scalar(out=freq[:, w : 2 * w], in0=freq[:, 0:w], scalar1=ratio ** w, scalar2=None, op0=ALU.mult)
+        turns = const.tile([P, 2, HALF], F32, name="turns")
+        for parity in range(2):
+            nc.vector.tensor_scalar(
+                out=turns[:, parity, :], in0=freq[:], scalar1=pos[:, parity : parity + 1], scalar2=None, op0=ALU.mult
+            )
+        turns_flat = turns[:].rearrange("p a c -> p (a c)")
+        whole_i = const.tile([P, P], I32, name="ki")
+        nc.vector.tensor_copy(out=whole_i[:], in_=turns_flat)
+        whole_f = const.tile([P, P], F32, name="kf")
+        nc.vector.tensor_copy(out=whole_f[:], in_=whole_i[:])
+        rest = const.tile([P, 2, HALF], F32, name="fr")
+        nc.vector.tensor_tensor(out=rest[:].rearrange("p a c -> p (a c)"), in0=turns_flat, in1=whole_f[:], op=ALU.subtract)
+        phase = const.tile([P, 2, 4, HALF], F32, name="ph")
+        for blk, shift in enumerate((0.25, 0.5, 0.0, 0.25)):
+            nc.vector.tensor_scalar(out=phase[:, :, blk, :], in0=rest[:], scalar1=shift, scalar2=None, op0=ALU.add)
+        phase_flat = phase[:].rearrange("p a b c -> p (a b c)")
+        wrapped = const.tile([P, 512], F32, name="gm")
+        nc.vector.scalar_tensor_tensor(out=wrapped[:], in0=phase_flat, scalar=0.5, in1=phase_flat, op0=ALU.is_gt, op1=ALU.subtract)
+        tables = const.tile([P, 2, 2, P], F32, name="cs")
 
         def tables_on_scalar():
-            nc.scalar.activation(out=cs[:].rearrange("p a b c -> p (a b c)"), in_=gm[:], func=ACT.Sin, scale=-2.0 * math.pi)
-            nc.scalar.activation(out=warm[:], in_=one[:], func=(ACT.Abs_reciprocal_sqrt if RSQRT_ON_SCALAR else ACT.Sqrt))
+            nc.scalar.activation(
+                out=tables[:].rearrange("p a b c -> p (a b c)"), in_=wrapped[:], func=ACT.Sin, scale=-2.0 * math.pi
+            )
+            nc.scalar.activation(out=warm[:], in_=one[:], func=ACT.Abs_reciprocal_sqrt)
 
-        xq, xs, gxs = [], [], {}
+        x_codes, x_scales, x_work = [], [], {}
 
         def x_transpose(m):
             words = xraw[m][:].bitcast(F32)
-            banks = []
-            for cp in range(2):
+            word_banks = []
+            for pass_pair in range(2):
                 xt = psum.tile([P, 2, 2, P], F32, name="xt", tag="aux", bufs=2)
                 for cc in range(2):
-                    c = 2 * cp + cc
+                    c = 2 * pass_pair + cc
                     for u in range(2):
                         nc.tensor.transpose(out=xt[:, cc, u, :], in_=words[:, 256 * c + u : 256 * (c + 1) : 2], identity=ident[:])
-                banks.append(xt)
-            gx = xpool.tile([P, 4, P, 4], BF16, name="gx", tag="gx", bufs=2, align_bytes=64)
-            gxs[m] = (gx, banks)
+                word_banks.append(xt)
+            x_grouped = xpool.tile([P, PASSES, P, PACK], BF16, name="gx", tag="gx", bufs=2, align_bytes=64)
+            x_work[m] = (x_grouped, word_banks)
 
-        def x_copy(m, cp, eng_copy):
-            gx, banks = gxs[m]
-            gw = gx[:].rearrange("p c r t -> p (c r t)").bitcast(F32).rearrange("p (c r u) -> p c r u", c=4, u=2)
-            eng_copy(out=gw[:, 2 * cp : 2 * cp + 2, :, :], in_=banks[cp][:].rearrange("p c u r -> p c r u"))
+        def x_copy(m, pass_pair, copy):
+            x_grouped, word_banks = x_work[m]
+            as_words = x_grouped[:].rearrange("p c r t -> p (c r t)").bitcast(F32).rearrange("p (c r u) -> p c r u", c=PASSES, u=2)
+            copy(
+                out=as_words[:, 2 * pass_pair : 2 * pass_pair + 2, :, :],
+                in_=word_banks[pass_pair][:].rearrange("p c u r -> p c r u"),
+            )
 
-        def x_quant(m):
-            gx, banks = gxs[m]
-            q = xpool.tile([P, 512], U32, name="xq%d" % m, align_bytes=64)
-            s = xpool.tile([P, 512], U8, name="xs%d" % m, align_bytes=64)
-            nc.vector.quantize_mx(out=q[:].bitcast(FP8X4), scales=s[:], in_=gx[:].rearrange("p c r t -> p (c r t)"))
-            xq.append(q)
-            xs.append(s)
+        def x_quantize(m):
+            x_grouped = x_work[m][0]
+            codes = xpool.tile([P, PASSES * P], U32, name="xq%d" % m, align_bytes=64)
+            scales = xpool.tile([P, PASSES * P], U8, name="xs%d" % m, align_bytes=64)
+            nc.vector.quantize_mx(out=codes[:].bitcast(FP8X4), scales=scales[:], in_=x_grouped[:].rearrange("p c r t -> p (c r t)"))
+            x_codes.append(codes)
+            x_scales.append(scales)
 
-        grouped, wq, ws, acc = {}, {}, {}, {}
+        grouped, w_codes, w_scales, sums, through = {}, {}, {}, {}, {}
 
-        def v_cols(k):
-            return V_HEAD if k < 5 else (V_LAST if k >= 28 else V_STEADY)
+        def vector_cols(k):
+            return VECTOR_COLS if k <= LAST_VECTOR_TILE else 0
 
-        def pt_cols(k):
-            return PT_COLS if PT_FIRST <= k < N_TILES else 0
+        def tensor_cols(k):
+            return TENSOR_COLS if FIRST_TENSOR_TILE <= k < W_TILES else 0
 
-        pts = {}
-
-        def pass_through(k):
-            w = pt_cols(k)
-            if w == 0:
+        def interleave_on_tensor(k):
+            width = tensor_cols(k)
+            if width == 0:
                 return
-            t, off = raw_of(k)
-            pt = psum.tile([P, 256, 4], BF16, name="pt", tag="aux", bufs=2)
-            for w0 in range(0, w, 128):
-                w1 = min(w, w0 + 128)
+            rows, col0 = raw_of(k)
+            first = col0 + BLOCK - width
+            pt = psum.tile([P, 256, PACK], BF16, name="pt", tag="aux", bufs=2)
+            for w0 in range(0, width, P):
+                w1 = min(width, w0 + P)
                 nc.tensor.matmul(
                     out=pt[:, w0:w1, :],
                     lhsT=identb[:],
-                    rhs=t[:, :, off + 512 - w + w0 : off + 512 - w + w1].rearrange("p j w -> p w j"),
+                    rhs=rows[:, :, first + w0 : first + w1].rearrange("p j w -> p w j"),
                     start=True,
                     stop=True,
                 )
-            pts[k] = pt
+            through[k] = pt
 
-        def pt_evacuate(k):
-            w = pt_cols(k)
-            if w == 0:
-                return
-            if k not in grouped:
-                grouped[k] = grp.tile([P, 512, 4], BF16, name="grouped", tag="grouped", align_bytes=64)
-            if PT_ON_VECTOR:
-                nc.vector.tensor_copy(out=grouped[k][:, 512 - w : 512, :], in_=pts[k][:, 0:w, :])
-            else:
-                nc.scalar.copy(out=grouped[k][:, 512 - w : 512, :], in_=pts[k][:, 0:w, :])
+        def new_grouped(k):
+            grouped[k] = grp.tile([P, BLOCK, PACK], BF16, name="grouped", tag="grouped", align_bytes=64)
 
-        def interleave(k, on_vector):
-            if k not in grouped:
-                grouped[k] = grp.tile([P, 512, 4], BF16, name="grouped", tag="grouped", align_bytes=64)
-            t, off = raw_of(k)
-            v = v_cols(k)
-            lo, hi = (0, v) if on_vector else (v, 512 - pt_cols(k))
-            if hi <= lo:
+        def interleave_on_scalar(k):
+            rows, col0 = raw_of(k)
+            lo, hi = vector_cols(k), BLOCK - tensor_cols(k)
+            nc.scalar.copy(out=grouped[k][:, lo:hi, :], in_=rows[:, :, col0 + lo : col0 + hi].rearrange("p j w -> p w j"))
+
+        def interleave_on_vector(k):
+            hi = vector_cols(k)
+            if hi == 0:
                 return
-            src = t[:, :, off + lo : off + hi].rearrange("p j w -> p w j")
-            if on_vector:
-                nc.vector.tensor_copy(out=grouped[k][:, lo:hi, :], in_=src)
-            else:
-                nc.scalar.copy(out=grouped[k][:, lo:hi, :], in_=src)
+            rows, col0 = raw_of(k)
+            nc.vector.tensor_copy(out=grouped[k][:, 0:hi, :], in_=rows[:, :, col0 : col0 + hi].rearrange("p j w -> p w j"))
+
+        def copy_from_tensor(k):
+            width = tensor_cols(k)
+            if width == 0:
+                return
+            nc.vector.tensor_copy(out=grouped[k][:, BLOCK - width : BLOCK, :], in_=through[k][:, 0:width, :])
 
         def quantize(k):
-            wq[k] = wqp.tile([P, 512], U32, name="wq", tag="wq", align_bytes=64)
-            ws[k] = wqp.tile([P, 512], U8, name="ws", tag="ws", align_bytes=64)
-            nc.vector.quantize_mx(out=wq[k][:].bitcast(FP8X4), scales=ws[k][:], in_=grouped[k][:].rearrange("p w j -> p (w j)"))
+            w_codes[k] = wqp.tile([P, BLOCK], U32, name="wq", tag="wq", align_bytes=64)
+            w_scales[k] = wqp.tile([P, BLOCK], U8, name="ws", tag="ws", align_bytes=64)
+            nc.vector.quantize_mx(
+                out=w_codes[k][:].bitcast(FP8X4), scales=w_scales[k][:], in_=grouped[k][:].rearrange("p w j -> p (w j)")
+            )
 
         def one_pass(k, m):
-            n, c = divmod(k, 4)
-            e = 4 * n + m
+            n, c = divmod(k, PASSES)
+            e = TOKEN_TILES * n + m
             if c == 0:
-                acc[e] = psum.tile([P, 512], F32, name="acc", tag="acc")
+                sums[e] = psum.tile([P, BLOCK], F32, name="acc", tag="acc")
             nc.tensor.matmul_mx(
-                out=acc[e][:],
-                lhsT=xq[m][:, P * c : P * (c + 1)].bitcast(FP8X4),
-                lhsT_scale=xs[m][:, P * c : P * (c + 1)],
-                rhs=wq[k][:].bitcast(FP8X4),
-                rhs_scale=ws[k][:],
+                out=sums[e][:],
+                lhsT=x_codes[m][:, P * c : P * (c + 1)].bitcast(FP8X4),
+                lhsT_scale=x_scales[m][:, P * c : P * (c + 1)],
+                rhs=w_codes[k][:].bitcast(FP8X4),
+                rhs_scale=w_scales[k][:],
                 start=(c == 0),
-                stop=(c == 3),
+                stop=(c == PASSES - 1),
             )
 
-        def passes(j):
-            c = j % 4
+        def passes(k):
+            c = k % PASSES
             for m in range(c):
-                one_pass(j, m)
+                one_pass(k, m)
             for cc in range(c + 1):
-                one_pass(j - c + cc, c)
+                one_pass(k - c + cc, c)
 
-        rts, rs, abs_ = {}, {}, {}
+        factors, products = {}, {}
 
-        def stats(e):
-            ss = small.tile([P, 4], F32, name="ss", tag="ss")
-            for h in range(4):
-                junk = small.tile([P, P], BF16, name="junk", tag="junk", bufs=2)
-                nc.scalar.activation(out=junk[:], in_=acc[e][:, P * h : P * (h + 1)], func=ACT.Square, accum_out=ss[:, h : h + 1])
-            rts[e] = small.tile([P, 4], F32, name="rt", tag="rt")
-            nc.scalar.activation(
-                out=rts[e][:], in_=ss[:], func=(ACT.Abs_reciprocal_sqrt if RSQRT_ON_SCALAR else ACT.Sqrt), scale=1.0 / 128.0, bias=EPS
-            )
-
-        def recip(e):
-            if RSQRT_ON_SCALAR:
-                rs[e] = rts[e]
-                return
-            rs[e] = small.tile([P, 4], F32, name="r", tag="r")
-            nc.vector.reciprocal(out=rs[e][:], in_=rts[e][:])
-
-        def rope(e, gated):
-            tt = e % 2
-            ab = epi.tile([P, 4, 2, P], F32, name="ab", tag="ab")
-            for h in range(3 if gated else 4):
-                nc.vector.scalar_tensor_tensor(
-                    out=ab[:, h, :, :],
-                    in0=acc[e][:, P * h : P * (h + 1)].unsqueeze(1).to_broadcast([P, 2, P]),
-                    scalar=rs[e][:, h : h + 1],
-                    in1=cs[:, tt, :, :],
-                    op0=ALU.mult,
-                    op1=ALU.mult,
+        def squares(e):
+            sumsq = small.tile([P, HEADS_IN_BANK], F32, name="ss", tag="ss")
+            for h in range(HEADS_IN_BANK):
+                unused = small.tile([P, P], BF16, name="junk", tag="junk", bufs=2)
+                nc.scalar.activation(
+                    out=unused[:], in_=sums[e][:, P * h : P * (h + 1)], func=ACT.Square, accum_out=sumsq[:, h : h + 1]
                 )
-            abs_[e] = ab
-            if gated:
-                rope_piece(e, 0, 0, P)
-                if ADD_HALF:
-                    rope_piece(e, 1, 64, P)
+            factors[e] = small.tile([P, HEADS_IN_BANK], F32, name="rt", tag="rt")
+            nc.scalar.activation(out=factors[e][:], in_=sumsq[:], func=ACT.Abs_reciprocal_sqrt, scale=1.0 / P, bias=EPS)
 
-        def rope_piece(e, plane, lo, hi):
+        def multiply_head(e, h):
             nc.vector.scalar_tensor_tensor(
-                out=abs_[e][:, 3, plane, lo:hi],
-                in0=acc[e][:, P * 3 + lo : P * 3 + hi],
-                scalar=rs[e][:, 3:4],
-                in1=cs[:, e % 2, plane, lo:hi],
+                out=products[e][:, h, :, :],
+                in0=sums[e][:, P * h : P * (h + 1)].unsqueeze(1).to_broadcast([P, 2, P]),
+                scalar=factors[e][:, h : h + 1],
+                in1=tables[:, e % 2, :, :],
                 op0=ALU.mult,
                 op1=ALU.mult,
             )
 
-        os_ = {}
-
-        def add_low(e, eng):
-            os_[e] = epi.tile([P, 4, P], F32, name="o", tag="o", bufs=4)
-            ab = abs_[e]
-            eng.tensor_tensor(out=os_[e][:, :, 0:64], in0=ab[:, :, 0, 0:64], in1=ab[:, :, 1, 64:128], op=ALU.add)
-
-        def add_store(e, with_low=True):
-            n, m = divmod(e, 4)
-            ab = abs_[e]
-            eng = nc.gpsimd if ADD_ON_GPSIMD else nc.vector
-            if with_low:
-                add_low(e, eng)
-            o = os_[e]
-            eng.tensor_tensor(out=o[:, :, 64:128], in0=ab[:, :, 0, 64:128], in1=ab[:, :, 1, 0:64], op=ALU.add)
-            b, t0, h0 = m // 2, P * (m % 2), 4 * (n % 4)
-            nc.sync.dma_start(
-                out=outs[n // 4][b, h0 : h0 + 4, t0 : t0 + P, :].rearrange("h t d -> t h d"),
-                in_=o[:],
+        def multiply_row(e, h, row):
+            nc.vector.scalar_tensor_tensor(
+                out=products[e][:, h, row, 0:P],
+                in0=sums[e][:, P * h : P * (h + 1)],
+                scalar=factors[e][:, h : h + 1],
+                in1=tables[:, e % 2, row, 0:P],
+                op0=ALU.mult,
+                op1=ALU.mult,
             )
 
-        for k in range(N_TILES + 6):
-            if 1 <= k <= 4:
-                load_w(("pair", 1, k - 1), k - 1, 1024, 1024)
-            if 5 <= k <= 8:
-                load_w(("pair", 2, k - 5), k - 5, 2048, 1024)
-            if 13 <= k <= 16:
-                load_w(("pair", 3, k - 13), k - 13, 3072, 1024)
-            if k < 4:
-                x_transpose(k)
-            pass_through(k + 1)
-            if 1 <= k <= N_TILES:
-                quantize(k - 1)
-                passes(k - 1)
-            if k < N_TILES:
-                if not PT_ON_VECTOR:
-                    pt_evacuate(k)
-                interleave(k, False)
-            if k < 4:
-                x_copy(k, 0, nc.scalar.copy)
-            if k == 2:
+        def add_and_store(e, engine):
+            n, m = divmod(e, TOKEN_TILES)
+            halves = products[e][:].rearrange("p h a (two i) -> p (h a) two i", two=2)
+            result = epi.tile([P, HEADS_IN_BANK, P], F32, name="o", tag="o", bufs=6)
+            engine.tensor_tensor(
+                out=result[:].rearrange("p h (a i) -> p (h a) i", a=2), in0=halves[:, :, 0, :], in1=halves[:, :, 1, :], op=ALU.add
+            )
+            b, t0, h0 = m // 2, P * (m % 2), HEADS_IN_BANK * (n % 4)
+            nc.sync.dma_start(
+                out=outs[n // 4][b, h0 : h0 + HEADS_IN_BANK, t0 : t0 + P, :].rearrange("h t d -> t h d"),
+                in_=result[:],
+            )
+
+        last_head = HEADS_IN_BANK - 1
+        for step in range(W_TILES + ADD_LAG):
+            for i, first_step in enumerate(PAIR_LOAD_STEPS):
+                if 0 <= step - first_step < PASSES:
+                    load_w(("pair", i + 1, step - first_step), step - first_step, 2 * BLOCK * (i + 1), 2 * BLOCK)
+            if step < TOKEN_TILES:
+                x_transpose(step)
+            interleave_on_tensor(step + 1)
+            if 1 <= step <= W_TILES:
+                quantize(step - 1)
+                passes(step - 1)
+            if step < W_TILES:
+                new_grouped(step)
+                interleave_on_scalar(step)
+            if step < TOKEN_TILES:
+                x_copy(step, 0, nc.scalar.copy)
+            if step == 2:
                 tables_on_scalar()
-            if k < N_TILES:
-                interleave(k, True)
-            if k < 4:
-                x_copy(k, 1, nc.vector.tensor_copy)
-            if ADD_ON_GPSIMD:
-                if 0 <= k - 6 < N_TILES:
-                    if ADD_HALF:
-                        add_low(k - 6, nc.vector)
-                        rope_piece(k - 6, 1, 0, 64)
-                        add_store(k - 6, False)
-                    else:
-                        rope_piece(k - 6, 1, 0, P)
-                        add_store(k - 6)
-                if 0 <= k - 5 < N_TILES:
-                    recip(k - 5)
-            else:
-                if 0 <= k - 5 < N_TILES:
-                    recip(k - 5)
-                if 0 <= k - 6 < N_TILES:
-                    add_store(k - 6)
-            if 0 <= k - 4 < N_TILES:
-                stats(k - 4)
-            if k < N_TILES and PT_ON_VECTOR:
-                pt_evacuate(k)
-            if 0 <= k - 5 < N_TILES:
-                rope(k - 5, ADD_ON_GPSIMD)
-            if k < 4:
-                x_quant(k)
+            if step < W_TILES:
+                interleave_on_vector(step)
+            if step < TOKEN_TILES:
+                x_copy(step, 1, nc.vector.tensor_copy)
+            if 0 <= step - ADD_LAG < BANKS - 1:
+                multiply_row(step - ADD_LAG, last_head, 1)
+                add_and_store(step - ADD_LAG, nc.gpsimd)
+            if 0 <= step - SQUARES_LAG < BANKS:
+                squares(step - SQUARES_LAG)
+            if step < W_TILES:
+                copy_from_tensor(step)
+            e = step - PRODUCTS_LAG
+            if 0 <= e < BANKS:
+                products[e] = epi.tile([P, HEADS_IN_BANK, 2, P], F32, name="ab", tag="ab")
+                for h in range(last_head):
+                    multiply_head(e, h)
+                if e < BANKS - 1:
+                    multiply_row(e, last_head, 0)
+                else:
+                    multiply_head(e, last_head)
+                    add_and_store(e, nc.vector)
+            if step < TOKEN_TILES:
+                x_quantize(step)

@@ -190,7 +190,10 @@ def tile_attn_pa_kernel(tc, x, W_qk, out_0, out_1):
         def interleave_on_scalar(k):
             rows, col0 = raw_of(k)
             lo, hi = vector_cols(k), BLOCK - tensor_cols(k)
-            nc.scalar.copy(out=grouped[k][:, lo:hi, :], in_=rows[:, :, col0 + lo : col0 + hi].rearrange("p j w -> p w j"))
+            nc.scalar.copy(
+                out=grouped[k][:, lo:hi, :].rearrange("p (c i) j -> p c j i", i=4),
+                in_=rows[:, :, col0 + lo : col0 + hi].rearrange("p j (c i) -> p c j i", i=4),
+            )
 
         def interleave_on_vector(k):
             hi = vector_cols(k)

@@ -49,7 +49,7 @@ def tile_attn_pa_kernel(tc, x, W_qk, out_0, out_1):
         const = ctx.enter_context(tc.tile_pool(name="const", bufs=1))
         xpool = ctx.enter_context(tc.tile_pool(name="xpool", bufs=1))
         rawp = ctx.enter_context(tc.tile_pool(name="rawp", bufs=8))
-        grp = ctx.enter_context(tc.tile_pool(name="grp", bufs=3))
+        grp = ctx.enter_context(tc.tile_pool(name="grp", bufs=4))
         wqp = ctx.enter_context(tc.tile_pool(name="wqp", bufs=5))
         small = ctx.enter_context(tc.tile_pool(name="small", bufs=4))
         epi = ctx.enter_context(tc.tile_pool(name="epi", bufs=3))
@@ -283,7 +283,7 @@ def tile_attn_pa_kernel(tc, x, W_qk, out_0, out_1):
             )
 
         last_head = HEADS_IN_BANK - 1
-        for step in range(W_TILES + ADD_LAG):
+        for step in range(W_TILES + PRODUCTS_LAG):
             for i, first_step in enumerate(PAIR_LOAD_STEPS):
                 if 0 <= step - first_step < PASSES:
                     load_w(("pair", i + 1, step - first_step), step - first_step, 2 * BLOCK * (i + 1), 2 * BLOCK)
@@ -293,9 +293,10 @@ def tile_attn_pa_kernel(tc, x, W_qk, out_0, out_1):
             if 1 <= step <= W_TILES:
                 quantize(step - 1)
                 passes(step - 1)
-            if step < W_TILES:
-                new_grouped(step)
-                interleave_on_scalar(step)
+            for k in (step,) if step < SQUARES_LAG else ((step, step + 1) if step == SQUARES_LAG else (step + 1,)):
+                if k < W_TILES:
+                    new_grouped(k)
+                    interleave_on_scalar(k)
             if step < TOKEN_TILES:
                 x_copy(step, 0, nc.scalar.copy)
             if step == 2:
@@ -304,9 +305,6 @@ def tile_attn_pa_kernel(tc, x, W_qk, out_0, out_1):
                 interleave_on_vector(step)
             if step < TOKEN_TILES:
                 x_copy(step, 1, nc.vector.tensor_copy)
-            if 0 <= step - ADD_LAG < BANKS - 1:
-                multiply_row(step - ADD_LAG, last_head, 1)
-                add_and_store(step - ADD_LAG, nc.gpsimd)
             if 0 <= step - SQUARES_LAG < BANKS:
                 squares(step - SQUARES_LAG)
             if step < W_TILES:
@@ -314,12 +312,8 @@ def tile_attn_pa_kernel(tc, x, W_qk, out_0, out_1):
             e = step - PRODUCTS_LAG
             if 0 <= e < BANKS:
                 products[e] = epi.tile([P, HEADS_IN_BANK, 2, P], F32, name="ab", tag="ab")
-                for h in range(last_head):
+                for h in range(HEADS_IN_BANK):
                     multiply_head(e, h)
-                if e < BANKS - 1:
-                    multiply_row(e, last_head, 0)
-                else:
-                    multiply_head(e, last_head)
-                    add_and_store(e, nc.vector)
+                add_and_store(e, nc.gpsimd if e < BANKS - 1 else nc.vector)
             if step < TOKEN_TILES:
                 x_quantize(step)

@@ -49,7 +49,7 @@ def tile_attn_pa_kernel(tc, x, W_qk, out_0, out_1):
         const = ctx.enter_context(tc.tile_pool(name="const", bufs=1))
         xpool = ctx.enter_context(tc.tile_pool(name="xpool", bufs=1))
         rawp = ctx.enter_context(tc.tile_pool(name="rawp", bufs=8))
-        grp = ctx.enter_context(tc.tile_pool(name="grp", bufs=4))
+        grp = ctx.enter_context(tc.tile_pool(name="grp", bufs=3))
         wqp = ctx.enter_context(tc.tile_pool(name="wqp", bufs=5))
         small = ctx.enter_context(tc.tile_pool(name="small", bufs=4))
         epi = ctx.enter_context(tc.tile_pool(name="epi", bufs=3))
@@ -293,10 +293,9 @@ def tile_attn_pa_kernel(tc, x, W_qk, out_0, out_1):
             if 1 <= step <= W_TILES:
                 quantize(step - 1)
                 passes(step - 1)
-            for k in (step,) if step < SQUARES_LAG else ((step, step + 1) if step == SQUARES_LAG else (step + 1,)):
-                if k < W_TILES:
-                    new_grouped(k)
-                    interleave_on_scalar(k)
+            if step < W_TILES:
+                new_grouped(step)
+                interleave_on_scalar(step)
             if step < TOKEN_TILES:
                 x_copy(step, 0, nc.scalar.copy)
             if step == 2:

@@ -191,8 +191,8 @@ def tile_attn_pa_kernel(tc, x, W_qk, out_0, out_1):
             rows, col0 = raw_of(k)
             lo, hi = vector_cols(k), BLOCK - tensor_cols(k)
             nc.scalar.copy(
-                out=grouped[k][:, lo:hi, :].rearrange("p (c i) j -> p c j i", i=4),
-                in_=rows[:, :, col0 + lo : col0 + hi].rearrange("p j (c i) -> p c j i", i=4),
+                out=grouped[k][:, lo:hi, :].rearrange("p (c i) j -> p c j i", i=8),
+                in_=rows[:, :, col0 + lo : col0 + hi].rearrange("p j (c i) -> p c j i", i=8),
             )
 
         def interleave_on_vector(k):

@@ -28,7 +28,7 @@ BANKS = 32
 EPS = 1e-6
 ROPE_BASE = 10000.0
 
-TENSOR_COLS = 240
+TENSOR_COLS = 232
 FIRST_TENSOR_TILE = 5
 VECTOR_COLS = 192
 LAST_VECTOR_TILE = 4
@@ -269,16 +269,16 @@ def tile_attn_pa_kernel(tc, x, W_qk, out_0, out_1):
                 op1=ALU.mult,
             )
 
-        def add_and_store(e, engine):
+        def add_and_store(e, engine, h_lo=0, h_hi=HEADS_IN_BANK):
             n, m = divmod(e, TOKEN_TILES)
-            halves = products[e][:].rearrange("p h a (two i) -> p (h a) two i", two=2)
-            result = epi.tile([P, HEADS_IN_BANK, P], F32, name="o", tag="o", bufs=6)
+            halves = products[e][:, h_lo:h_hi, :, :].rearrange("p h a (two i) -> p (h a) two i", two=2)
+            result = epi.tile([P, h_hi - h_lo, P], F32, name="o", tag="o", bufs=6)
             engine.tensor_tensor(
                 out=result[:].rearrange("p h (a i) -> p (h a) i", a=2), in0=halves[:, :, 0, :], in1=halves[:, :, 1, :], op=ALU.add
             )
             b, t0, h0 = m // 2, P * (m % 2), HEADS_IN_BANK * (n % 4)
             nc.sync.dma_start(
-                out=outs[n // 4][b, h0 : h0 + HEADS_IN_BANK, t0 : t0 + P, :].rearrange("h t d -> t h d"),
+                out=outs[n // 4][b, h0 + h_lo : h0 + h_hi, t0 : t0 + P, :].rearrange("h t d -> t h d"),
                 in_=result[:],
             )
 
@@ -292,7 +292,6 @@ def tile_attn_pa_kernel(tc, x, W_qk, out_0, out_1):
             interleave_on_tensor(step + 1)
             if 1 <= step <= W_TILES:
                 quantize(step - 1)
-                passes(step - 1)
             if step < W_TILES:
                 new_grouped(step)
                 interleave_on_scalar(step)
@@ -302,6 +301,10 @@ def tile_attn_pa_kernel(tc, x, W_qk, out_0, out_1):
                 tables_on_scalar()
             if step < W_TILES:
                 interleave_on_vector(step)
+            if 1 <= step <= TOKEN_TILES:
+                x_quantize(step - 1)
+            if 1 <= step <= W_TILES:
+                passes(step - 1)
             if step < TOKEN_TILES:
                 x_copy(step, 1, nc.vector.tensor_copy)
             if 0 <= step - SQUARES_LAG < BANKS:
@@ -311,8 +314,13 @@ def tile_attn_pa_kernel(tc, x, W_qk, out_0, out_1):
             e = step - PRODUCTS_LAG
             if 0 <= e < BANKS:
                 products[e] = epi.tile([P, HEADS_IN_BANK, 2, P], F32, name="ab", tag="ab")
-                for h in range(HEADS_IN_BANK):
-                    multiply_head(e, h)
-                add_and_store(e, nc.gpsimd if e < BANKS - 1 else nc.vector)
-            if step < TOKEN_TILES:
-                x_quantize(step)
+                if e < BANKS - 1:
+                    for h in range(HEADS_IN_BANK):
+                        multiply_head(e, h)
+                    add_and_store(e, nc.gpsimd)
+                else:
+                    for h in range(last_head):
+                        multiply_head(e, h)
+                    add_and_store(e, nc.vector, 0, 2)
+                    multiply_head(e, last_head)
+                    add_and_store(e, nc.vector, 2, HEADS_IN_BANK)

from contextlib import ExitStack
import math

import concourse.mybir as mybir
from concourse.masks import make_identity

FLOPS = 2 * 512 * 2048 * 4096

F32 = mybir.dt.float32
BF16 = mybir.dt.bfloat16
U32 = mybir.dt.uint32
U8 = mybir.dt.uint8
I32 = mybir.dt.int32
FP8X4 = mybir.dt.float8_e5m2_x4
ALU = mybir.AluOpType
ACT = mybir.ActivationFunctionType

P = 128
HALF = 64
PACK = 4
K_PASS = P * PACK
PASSES = 4
BLOCK = 512
HEADS_IN_BANK = 4
TOKEN_TILES = 4
W_TILES = 32
BANKS = 32
EPS = 1e-6
ROPE_BASE = 10000.0

TENSOR_COLS = 232
FIRST_TENSOR_TILE = 5
VECTOR_COLS = 192
LAST_VECTOR_TILE = 4

SQUARES_LAG = 4
PRODUCTS_LAG = 5
ADD_LAG = 6

PAIR_LOAD_STEPS = (1, 9, 17)


def tile_attn_pa_kernel(tc, x, W_qk, out_0, out_1):
    nc = tc.nc
    xf = x.flatten_outer_dims()
    outs = (out_0, out_1)

    with ExitStack() as ctx:
        const = ctx.enter_context(tc.tile_pool(name="const", bufs=1))
        xpool = ctx.enter_context(tc.tile_pool(name="xpool", bufs=1))
        rawp = ctx.enter_context(tc.tile_pool(name="rawp", bufs=8))
        grp = ctx.enter_context(tc.tile_pool(name="grp", bufs=3))
        wqp = ctx.enter_context(tc.tile_pool(name="wqp", bufs=5))
        small = ctx.enter_context(tc.tile_pool(name="small", bufs=4))
        epi = ctx.enter_context(tc.tile_pool(name="epi", bufs=3))
        psum = ctx.enter_context(tc.psum_pool(name="psum", bufs=6))
        ctx.enter_context(tc.manual_schedule())

        xraw = []
        raw = {}

        def load_x(m):
            tokens = xpool.tile([P, 2048], BF16, name="xraw%d" % m)
            nc.sync.dma_start(out=tokens[:], in_=xf[P * m : P * (m + 1), :])
            xraw.append(tokens)

        def load_w(key, c, col0, width):
            rows = rawp.tile([P, PACK, width], BF16, name="raw", tag="raw")
            nc.sync.dma_start(
                out=rows[:],
                in_=W_qk[K_PASS * c : K_PASS * (c + 1), col0 : col0 + width].rearrange("(p j) w -> p j w", j=PACK),
            )
            raw[key] = rows

        for c in range(PASSES):
            load_w((0, c), c, 0, BLOCK)
            load_x(c)
        for c in range(PASSES):
            load_w((1, c), c, BLOCK, BLOCK)

        def raw_of(k):
            n, c = divmod(k, PASSES)
            if n < 2:
                return raw[(n, c)], 0
            return raw[("pair", n // 2, c)], BLOCK * (n % 2)

        ident = const.tile([P, P], F32, name="ident")
        make_identity(nc, ident[:])
        identb = const.tile([P, P], BF16, name="identb")
        nc.vector.tensor_copy(out=identb[:], in_=ident[:])

        pos = const.tile([P, 2], F32, name="pcol")
        nc.gpsimd.iota(pos[:], pattern=[[P, 2]], base=0, channel_multiplier=1, allow_small_or_imprecise_dtypes=True)
        one = const.tile([P, 1], F32, name="one")
        nc.vector.memset(one[:], 1.0)
        warm = const.tile([P, 1], F32, name="warm")
        nc.scalar.activation(out=warm[:], in_=one[:], func=ACT.Sin)
        freq = const.tile([P, HALF], F32, name="phi")
        nc.vector.tensor_scalar(out=freq[:, 0:1], in0=one[:], scalar1=1.0 / (2.0 * math.pi), scalar2=None, op0=ALU.mult)
        ratio = ROPE_BASE ** (-2.0 / P)
        for s in range(6):
            w = 2 ** s
            nc.vector.tensor_scalar(out=freq[:, w : 2 * w], in0=freq[:, 0:w], scalar1=ratio ** w, scalar2=None, op0=ALU.mult)
        turns = const.tile([P, 2, HALF], F32, name="turns")
        for parity in range(2):
            nc.vector.tensor_scalar(
                out=turns[:, parity, :], in0=freq[:], scalar1=pos[:, parity : parity + 1], scalar2=None, op0=ALU.mult
            )
        turns_flat = turns[:].rearrange("p a c -> p (a c)")
        whole_i = const.tile([P, P], I32, name="ki")
        nc.vector.tensor_copy(out=whole_i[:], in_=turns_flat)
        whole_f = const.tile([P, P], F32, name="kf")
        nc.vector.tensor_copy(out=whole_f[:], in_=whole_i[:])
        rest = const.tile([P, 2, HALF], F32, name="fr")
        nc.vector.tensor_tensor(out=rest[:].rearrange("p a c -> p (a c)"), in0=turns_flat, in1=whole_f[:], op=ALU.subtract)
        phase = const.tile([P, 2, 4, HALF], F32, name="ph")
        for blk, shift in enumerate((0.25, 0.5, 0.0, 0.25)):
            nc.vector.tensor_scalar(out=phase[:, :, blk, :], in0=rest[:], scalar1=shift, scalar2=None, op0=ALU.add)
        phase_flat = phase[:].rearrange("p a b c -> p (a b c)")
        wrapped = const.tile([P, 512], F32, name="gm")
        nc.vector.scalar_tensor_tensor(out=wrapped[:], in0=phase_flat, scalar=0.5, in1=phase_flat, op0=ALU.is_gt, op1=ALU.subtract)
        tables = const.tile([P, 2, 2, P], F32, name="cs")

        def tables_on_scalar():
            nc.scalar.activation(
                out=tables[:].rearrange("p a b c -> p (a b c)"), in_=wrapped[:], func=ACT.Sin, scale=-2.0 * math.pi
            )
            nc.scalar.activation(out=warm[:], in_=one[:], func=ACT.Abs_reciprocal_sqrt)

        x_codes, x_scales, x_work = [], [], {}

        def x_transpose(m):
            words = xraw[m][:].bitcast(F32)
            word_banks = []
            for pass_pair in range(2):
                xt = psum.tile([P, 2, 2, P], F32, name="xt", tag="aux", bufs=2)
                for cc in range(2):
                    c = 2 * pass_pair + cc
                    for u in range(2):
                        nc.tensor.transpose(out=xt[:, cc, u, :], in_=words[:, 256 * c + u : 256 * (c + 1) : 2], identity=ident[:])
                word_banks.append(xt)
            x_grouped = xpool.tile([P, PASSES, P, PACK], BF16, name="gx", tag="gx", bufs=2, align_bytes=64)
            x_work[m] = (x_grouped, word_banks)

        def x_copy(m, pass_pair, copy):
            x_grouped, word_banks = x_work[m]
            as_words = x_grouped[:].rearrange("p c r t -> p (c r t)").bitcast(F32).rearrange("p (c r u) -> p c r u", c=PASSES, u=2)
            copy(
                out=as_words[:, 2 * pass_pair : 2 * pass_pair + 2, :, :],
                in_=word_banks[pass_pair][:].rearrange("p c u r -> p c r u"),
            )

        def x_quantize(m):
            x_grouped = x_work[m][0]
            codes = xpool.tile([P, PASSES * P], U32, name="xq%d" % m, align_bytes=64)
            scales = xpool.tile([P, PASSES * P], U8, name="xs%d" % m, align_bytes=64)
            nc.vector.quantize_mx(out=codes[:].bitcast(FP8X4), scales=scales[:], in_=x_grouped[:].rearrange("p c r t -> p (c r t)"))
            x_codes.append(codes)
            x_scales.append(scales)

        grouped, w_codes, w_scales, sums, through = {}, {}, {}, {}, {}

        def vector_cols(k):
            return VECTOR_COLS if k <= LAST_VECTOR_TILE else 0

        def tensor_cols(k):
            return TENSOR_COLS if FIRST_TENSOR_TILE <= k < W_TILES else 0

        def interleave_on_tensor(k):
            width = tensor_cols(k)
            if width == 0:
                return
            rows, col0 = raw_of(k)
            first = col0 + BLOCK - width
            pt = psum.tile([P, 256, PACK], BF16, name="pt", tag="aux", bufs=2)
            for w0 in range(0, width, P):
                w1 = min(width, w0 + P)
                nc.tensor.matmul(
                    out=pt[:, w0:w1, :],
                    lhsT=identb[:],
                    rhs=rows[:, :, first + w0 : first + w1].rearrange("p j w -> p w j"),
                    start=True,
                    stop=True,
                )
            through[k] = pt

        def new_grouped(k):
            grouped[k] = grp.tile([P, BLOCK, PACK], BF16, name="grouped", tag="grouped", align_bytes=64)

        def interleave_on_scalar(k):
            rows, col0 = raw_of(k)
            lo, hi = vector_cols(k), BLOCK - tensor_cols(k)
            nc.scalar.copy(
                out=grouped[k][:, lo:hi, :].rearrange("p (c i) j -> p c j i", i=8),
                in_=rows[:, :, col0 + lo : col0 + hi].rearrange("p j (c i) -> p c j i", i=8),
            )

        def interleave_on_vector(k):
            hi = vector_cols(k)
            if hi == 0:
                return
            rows, col0 = raw_of(k)
            nc.vector.tensor_copy(out=grouped[k][:, 0:hi, :], in_=rows[:, :, col0 : col0 + hi].rearrange("p j w -> p w j"))

        def copy_from_tensor(k):
            width = tensor_cols(k)
            if width == 0:
                return
            nc.vector.tensor_copy(out=grouped[k][:, BLOCK - width : BLOCK, :], in_=through[k][:, 0:width, :])

        def quantize(k):
            w_codes[k] = wqp.tile([P, BLOCK], U32, name="wq", tag="wq", align_bytes=64)
            w_scales[k] = wqp.tile([P, BLOCK], U8, name="ws", tag="ws", align_bytes=64)
            nc.vector.quantize_mx(
                out=w_codes[k][:].bitcast(FP8X4), scales=w_scales[k][:], in_=grouped[k][:].rearrange("p w j -> p (w j)")
            )

        def one_pass(k, m):
            n, c = divmod(k, PASSES)
            e = TOKEN_TILES * n + m
            if c == 0:
                sums[e] = psum.tile([P, BLOCK], F32, name="acc", tag="acc")
            nc.tensor.matmul_mx(
                out=sums[e][:],
                lhsT=x_codes[m][:, P * c : P * (c + 1)].bitcast(FP8X4),
                lhsT_scale=x_scales[m][:, P * c : P * (c + 1)],
                rhs=w_codes[k][:].bitcast(FP8X4),
                rhs_scale=w_scales[k][:],
                start=(c == 0),
                stop=(c == PASSES - 1),
            )

        def passes(k):
            c = k % PASSES
            for m in range(c):
                one_pass(k, m)
            for cc in range(c + 1):
                one_pass(k - c + cc, c)

        factors, products = {}, {}

        def squares(e):
            sumsq = small.tile([P, HEADS_IN_BANK], F32, name="ss", tag="ss")
            for h in range(HEADS_IN_BANK):
                unused = small.tile([P, P], BF16, name="junk", tag="junk", bufs=2)
                nc.scalar.activation(
                    out=unused[:], in_=sums[e][:, P * h : P * (h + 1)], func=ACT.Square, accum_out=sumsq[:, h : h + 1]
                )
            factors[e] = small.tile([P, HEADS_IN_BANK], F32, name="rt", tag="rt")
            nc.scalar.activation(out=factors[e][:], in_=sumsq[:], func=ACT.Abs_reciprocal_sqrt, scale=1.0 / P, bias=EPS)

        def multiply_head(e, h):
            nc.vector.scalar_tensor_tensor(
                out=products[e][:, h, :, :],
                in0=sums[e][:, P * h : P * (h + 1)].unsqueeze(1).to_broadcast([P, 2, P]),
                scalar=factors[e][:, h : h + 1],
                in1=tables[:, e % 2, :, :],
                op0=ALU.mult,
                op1=ALU.mult,
            )

        def multiply_row(e, h, row):
            nc.vector.scalar_tensor_tensor(
                out=products[e][:, h, row, 0:P],
                in0=sums[e][:, P * h : P * (h + 1)],
                scalar=factors[e][:, h : h + 1],
                in1=tables[:, e % 2, row, 0:P],
                op0=ALU.mult,
                op1=ALU.mult,
            )

        def add_and_store(e, engine, h_lo=0, h_hi=HEADS_IN_BANK):
            n, m = divmod(e, TOKEN_TILES)
            halves = products[e][:, h_lo:h_hi, :, :].rearrange("p h a (two i) -> p (h a) two i", two=2)
            result = epi.tile([P, h_hi - h_lo, P], F32, name="o", tag="o", bufs=6)
            engine.tensor_tensor(
                out=result[:].rearrange("p h (a i) -> p (h a) i", a=2), in0=halves[:, :, 0, :], in1=halves[:, :, 1, :], op=ALU.add
            )
            b, t0, h0 = m // 2, P * (m % 2), HEADS_IN_BANK * (n % 4)
            nc.sync.dma_start(
                out=outs[n // 4][b, h0 + h_lo : h0 + h_hi, t0 : t0 + P, :].rearrange("h t d -> t h d"),
                in_=result[:],
            )

        last_head = HEADS_IN_BANK - 1
        for step in range(W_TILES + PRODUCTS_LAG):
            for i, first_step in enumerate(PAIR_LOAD_STEPS):
                if 0 <= step - first_step < PASSES:
                    load_w(("pair", i + 1, step - first_step), step - first_step, 2 * BLOCK * (i + 1), 2 * BLOCK)
            if step < TOKEN_TILES:
                x_transpose(step)
            interleave_on_tensor(step + 1)
            if 1 <= step <= W_TILES:
                quantize(step - 1)
            if step < W_TILES:
                new_grouped(step)
                interleave_on_scalar(step)
            if step < TOKEN_TILES:
                x_copy(step, 0, nc.scalar.copy)
            if step == 2:
                tables_on_scalar()
            if step < W_TILES:
                interleave_on_vector(step)
            if 1 <= step <= TOKEN_TILES:
                x_quantize(step - 1)
            if 1 <= step <= W_TILES:
                passes(step - 1)
            if step < TOKEN_TILES:
                x_copy(step, 1, nc.vector.tensor_copy)
            if 0 <= step - SQUARES_LAG < BANKS:
                squares(step - SQUARES_LAG)
            if step < W_TILES:
                copy_from_tensor(step)
            e = step - PRODUCTS_LAG
            if 0 <= e < BANKS:
                products[e] = epi.tile([P, HEADS_IN_BANK, 2, P], F32, name="ab", tag="ab")
                if e < BANKS - 1:
                    for h in range(HEADS_IN_BANK):
                        multiply_head(e, h)
                    add_and_store(e, nc.gpsimd)
                else:
                    for h in range(last_head):
                        multiply_head(e, h)
                    add_and_store(e, nc.vector, 0, 2)
                    multiply_head(e, last_head)
                    add_and_store(e, nc.vector, 2, HEADS_IN_BANK)
